import numpy as np
import ml_dtypes


def mxq(x, axis, fmt="e4m3"):
    dtype, down = {"e4m3": (ml_dtypes.float8_e4m3fn, 7), "e5m2": (ml_dtypes.float8_e5m2, 14)}[fmt]
    v = np.moveaxis(np.asarray(x, np.float32).astype(ml_dtypes.bfloat16).astype(np.float64), axis, -1)
    blocks = v.reshape(v.shape[:-1] + (-1, 32))
    amax = np.abs(blocks).max(-1, keepdims=True)
    byte = np.maximum(np.where(amax > 0, np.frexp(amax)[1] - 1 + 127, 0) - down, 1)
    scale = np.exp2(byte - 127.0)
    codes = (blocks / scale).astype(np.float32).astype(dtype).astype(np.float64)
    return np.moveaxis((codes * scale).reshape(v.shape), -1, axis)


WIDE = False


def mx_kscale(k):
    if not WIDE:
        return np.ones(k)
    levels = np.array([10, -10, 5, -5, 0])
    a = np.random.permutation(np.resize(levels, k // 512 * 4)).reshape(k // 512, 4)
    idx = np.arange(k)
    return np.exp2(a[idx // 512, idx % 128 // 32])


BF16 = ml_dtypes.bfloat16


def bf(x):
    return np.asarray(x, np.float32).astype(BF16)


def f64(x):
    return np.asarray(x).astype(np.float64)


B, I, M, O = 8192, 6, 4, 128
R = M ** I
NW = I // 2
EPS = 1e-6
C = 2.0 ** -14


def setup_inputs():
    x = np.random.standard_normal((B, I)) * np.sqrt(24.0 / I) * C
    means = np.random.standard_normal((I, M)) * 0.5 * C
    sign = np.where(np.random.standard_normal((I, M)) < 0.0, -1.0, 1.0)
    sigmas = sign * (0.85 + 0.3 * np.random.random((I, M))) * C
    rules = np.random.standard_normal((R, O)) * 4.0
    lv = np.unique(np.log2(mx_kscale(R)))
    e = lv[np.arange(NW * M) % len(lv)].reshape(NW, M)
    a = e.max(axis=1, keepdims=True) - e
    wide = len(lv) > 1
    sigmas[:NW] *= 32.0 if wide else 1.0
    means[:NW] += np.sqrt(2.0 * np.log(2.0) * a) * (np.abs(sigmas[:NW]) + EPS)
    A = np.zeros(1)
    for i in range(NW):
        A = (A[:, None] + a[i][None, :]).reshape(-1)
    rules = rules * np.exp2(np.repeat(A, R // len(A)))[:, None] / (np.sqrt(len(A)) if wide else 1.0)
    return {"x": bf(x), "mfs": bf(np.stack([means, sigmas], axis=2)), "rules": bf(rules)}


def reference(x, mfs, rules):
    x, mfs = f64(x), f64(mfs)
    means = mfs[:, :, 0]
    sigmas = np.abs(mfs[:, :, 1]) + EPS
    z = (x[:, :, None] - means[None]) / sigmas[None]
    memb = np.exp(-0.5 * z * z)
    nb = x.shape[0]
    strengths = np.ones((nb, 1))
    for i in range(I):
        strengths = (strengths[:, :, None] * memb[:, i, None, :]).reshape(nb, -1)
    norm = strengths / (np.sum(strengths, axis=1, keepdims=True) + EPS)
    return mxq(norm, 1, "e4m3") @ mxq(f64(rules), 0, "e4m3")

@@ -1,0 +1,254 @@
+from contextlib import ExitStack
+
+import concourse.mybir as mybir
+from concourse.masks import make_identity
+
+F32 = mybir.dt.float32
+BF16 = mybir.dt.bfloat16
+U32 = mybir.dt.uint32
+U8 = mybir.dt.uint8
+FP8X4 = mybir.dt.float8_e4m3fn_x4
+ALU = mybir.AluOpType
+ACT = mybir.ActivationFunctionType
+AX = mybir.AxisListType
+
+P = 128
+B, I, M, O = 8192, 6, 4, 128
+R = M ** I
+NT = B // P
+CHUNKS = (2, 6, 8, 8, 8, 8, 8, 8, 8)
+PASSES = R // 512
+EPS = 1e-6
+FLOPS = 2 * B * R * O
+
+
+def scalar_share(j):
+    if j == 0:
+        return ()
+    if j % 2 == 0:
+        return (5, 10, 15)
+    return (3, 7, 11, 15)
+
+
+def tile_extendedanfis_kernel(tc, x, mfs, rules, out):
+    nc = tc.nc
+    n_chunks = len(CHUNKS)
+    starts = [sum(CHUNKS[:c]) for c in range(n_chunks)]
+    chunk_of = []
+    for c in range(n_chunks):
+        chunk_of.extend([c] * CHUNKS[c])
+    with ExitStack() as ctx:
+        ctx.enter_context(tc.manual_schedule())
+        const = ctx.enter_context(tc.tile_pool(name="const", bufs=1))
+        pro = ctx.enter_context(tc.tile_pool(name="pro", bufs=2))
+        tab = ctx.enter_context(tc.tile_pool(name="tab", bufs=2))
+        nbp = ctx.enter_context(tc.tile_pool(name="nbp", bufs=3))
+        grpp = ctx.enter_context(tc.tile_pool(name="grpp", bufs=3))
+        qp = ctx.enter_context(tc.tile_pool(name="qp", bufs=3))
+        outp = ctx.enter_context(tc.tile_pool(name="outp", bufs=2))
+        ps_t = ctx.enter_context(tc.psum_pool(name="ps_t", bufs=6))
+        ps_a = ctx.enter_context(tc.psum_pool(name="ps_a", bufs=2))
+
+        x_sb = const.tile([P, NT, I], BF16)
+        nc.sync.dma_start(out=x_sb[:], in_=x.rearrange("(p j) i -> p j i", j=NT))
+        mfb = const.tile([P, I, M, 2], BF16)
+        nc.scalar.dma_start(
+            out=mfb[:].rearrange("p i m c -> p (i m c)"),
+            in_=mfs.rearrange("i m c -> (i m c)").partition_broadcast(P),
+        )
+        rraw = const.tile([P, PASSES, 4, O], BF16)
+        nc.sync.dma_start(out=rraw[:], in_=rules.rearrange("(g p t) o -> p g t o", p=P, t=4))
+
+        ident = const.tile([P, P], F32)
+        make_identity(nc, ident[:])
+
+        mu = const.tile([P, I, M], F32)
+        nc.vector.tensor_copy(out=mu[:], in_=mfb[:, :, :, 0])
+        sg = const.tile([P, I, M], F32)
+        nc.scalar.activation(out=sg[:], in_=mfb[:, :, :, 1], func=ACT.Abs)
+        nc.vector.tensor_scalar_add(out=sg[:], in0=sg[:], scalar1=EPS)
+        rs = const.tile([P, I, M], F32)
+        nc.vector.reciprocal(out=rs[:], in_=sg[:])
+
+        out_v = out.rearrange("(p j) o -> p j o", j=NT)
+
+        def pro_a(c):
+            j0 = starts[c]
+            nj = CHUNKS[c]
+            full = [P, nj, I, M]
+            z = pro.tile(full, F32, tag="z")
+            nc.vector.tensor_tensor(
+                out=z[:],
+                in0=x_sb[:, j0 : j0 + nj, :].unsqueeze(3).to_broadcast(full),
+                in1=mu[:].unsqueeze(1).to_broadcast(full),
+                op=ALU.subtract,
+            )
+            nc.vector.tensor_tensor(out=z[:], in0=z[:], in1=rs[:].unsqueeze(1).to_broadcast(full), op=ALU.mult)
+            return z
+
+        def pro_b(c, z):
+            mb = pro.tile([P, CHUNKS[c], I, M], F32, tag="mb")
+            nc.scalar.activation(out=z[:], in_=z[:], func=ACT.Square)
+            nc.scalar.activation(out=mb[:], in_=z[:], func=ACT.Exp, scale=-0.5)
+            return mb
+
+        def pro_c(c, mb):
+            nj = CHUNKS[c]
+            ssum = pro.tile([P, nj, I], F32, tag="ssum")
+            nc.vector.tensor_reduce(out=ssum[:], in_=mb[:], axis=AX.X, op=ALU.add)
+            t3 = pro.tile([P, nj, 3], F32, tag="t3")
+            nc.vector.tensor_tensor(out=t3[:], in0=ssum[:, :, 0:3], in1=ssum[:, :, 3:6], op=ALU.mult)
+            den = pro.tile([P, nj, 1], F32, tag="den")
+            nc.vector.tensor_tensor(out=den[:], in0=t3[:, :, 0:1], in1=t3[:, :, 1:2], op=ALU.mult)
+            nc.vector.tensor_tensor(out=den[:], in0=den[:], in1=t3[:, :, 2:3], op=ALU.mult)
+            nc.vector.tensor_scalar_add(out=den[:], in0=den[:], scalar1=EPS)
+            rn = pro.tile([P, nj, 1], F32, tag="rn")
+            nc.vector.reciprocal(out=rn[:], in_=den[:])
+            m0n = pro.tile([P, nj, M], F32, tag="m0n")
+            nc.vector.tensor_tensor(out=m0n[:], in0=mb[:, :, 0, :], in1=rn[:].to_broadcast([P, nj, M]), op=ALU.mult)
+            sq = [P, nj, M, M]
+            s16 = tab.tile(sq, F32, tag="s16")
+            nc.vector.tensor_tensor(
+                out=s16[:],
+                in0=m0n[:].unsqueeze(3).to_broadcast(sq),
+                in1=mb[:, :, 1, :].unsqueeze(2).to_broadcast(sq),
+                op=ALU.mult,
+            )
+            p23 = pro.tile(sq, F32, tag="p23")
+            nc.vector.tensor_tensor(
+                out=p23[:],
+                in0=mb[:, :, 2, :].unsqueeze(3).to_broadcast(sq),
+                in1=mb[:, :, 3, :].unsqueeze(2).to_broadcast(sq),
+                op=ALU.mult,
+            )
+            p45 = pro.tile([P, nj, 2, M, 2], F32, tag="p45")
+            r4 = tab.tile([P, nj, 2, 16, 8], F32, tag="r4")
+            for u in range(2):
+                nc.vector.tensor_tensor(
+                    out=p45[:, :, u, :, :],
+                    in0=mb[:, :, 4, :].unsqueeze(3).to_broadcast([P, nj, M, 2]),
+                    in1=mb[:, :, 5, 2 * u : 2 * u + 2].unsqueeze(2).to_broadcast([P, nj, M, 2]),
+                    op=ALU.mult,
+                )
+            for u in range(2):
+                nc.vector.tensor_tensor(
+                    out=r4[:, :, u, :, :],
+                    in0=p23[:].rearrange("p j a b -> p j (a b)").unsqueeze(3).to_broadcast([P, nj, 16, 8]),
+                    in1=p45[:, :, u, :, :].rearrange("p j a b -> p j (a b)").unsqueeze(2).to_broadcast([P, nj, 16, 8]),
+                    op=ALU.mult,
+                )
+            return s16, r4
+
+        rgrp = const.tile([P, PASSES, O, 4], BF16, align_bytes=64)
+        rcodes = const.tile([P, PASSES * O], U32, align_bytes=64)
+        rscl = const.tile([P, PASSES * O], U8, align_bytes=64)
+
+        def rules_regroup():
+            for g in range(0, PASSES, 2):
+                nc.scalar.copy(out=rgrp[:, g : g + 2, :, :], in_=rraw[:, g : g + 2, :, :].rearrange("p g t o -> p g o t"))
+
+        def rules_quant():
+            nc.vector.quantize_mx(
+                out=rcodes[:].bitcast(FP8X4), scales=rscl[:], in_=rgrp[:].rearrange("p g o t -> p (g o t)")
+            )
+
+        tabs = {}
+        zs = {}
+        mbs = {}
+        nbs = {}
+        grps = {}
+        qs = {}
+        osbs = {}
+
+        def gen(j):
+            c = chunk_of[j]
+            s16, r4 = tabs[c]
+            jj = j - starts[c]
+            share = scalar_share(j)
+            nb = nbp.tile([P, PASSES, 2, 2, 128], BF16, tag="nb")
+            src = r4[:, jj, :, :, :].rearrange("p u a c -> p u (a c)")
+            for h in range(16):
+                dst = nb[:, h // 2, :, h % 2, :]
+                sc = s16[:, jj, h // 4, h % 4 : h % 4 + 1]
+                if h in share:
+                    nc.scalar.activation(out=dst, in_=src, func=ACT.Copy, scale=sc)
+                else:
+                    nc.vector.tensor_scalar_mul(out=dst, in0=src, scalar1=sc)
+            nbs[j] = nb
+
+        def trans(j):
+            nbw = nbs[j][:].rearrange("p g u s c -> p (g u s c)").bitcast(F32)
+            grp = grpp.tile([P, PASSES * P * 4], BF16, tag="grp", align_bytes=64)
+            gw = grp[:].bitcast(F32).rearrange("p (g b u) -> p g b u", g=PASSES, u=2)
+            xts = []
+            for q in range(4):
+                xt = ps_t.tile([P, 4, P], F32, tag="xt")
+                for r in range(4):
+                    blk = 4 * q + r
+                    nc.tensor.transpose(xt[:, r, :], nbw[:, blk * P : (blk + 1) * P], ident[:])
+                xts.append(xt)
+            for q in range(4):
+                nc.scalar.copy(
+                    out=gw[:, 2 * q : 2 * q + 2, :, :], in_=xts[q][:].rearrange("p (g u) b -> p g b u", u=2)
+                )
+            grps[j] = grp
+
+        def quant(j):
+            codes = qp.tile([P, PASSES * P], U32, tag="codes", align_bytes=64)
+            scl = qp.tile([P, PASSES * P], U8, tag="scl", align_bytes=64)
+            nc.vector.quantize_mx(out=codes[:].bitcast(FP8X4), scales=scl[:], in_=grps[j][:])
+            qs[j] = (codes, scl)
+
+        def mx(j):
+            codes, scl = qs[j]
+            acc = ps_a.tile([P, O], F32, tag="acc")
+            for g in range(PASSES):
+                cols = slice(g * P, (g + 1) * P)
+                nc.tensor.matmul_mx(
+                    out=acc[:],
+                    lhsT=codes[:, cols].bitcast(FP8X4),
+                    lhsT_scale=scl[:, cols],
+                    rhs=rcodes[:, cols].bitcast(FP8X4),
+                    rhs_scale=rscl[:, cols],
+                    start=(g == 0),
+                    stop=(g == PASSES - 1),
+                )
+            c = chunk_of[j]
+            jj = j - starts[c]
+            if jj == 0:
+                osb = outp.tile([P, CHUNKS[c], O], F32, tag="osb")
+                osbs[c] = osb
+            nc.scalar.copy(out=osbs[c][:, jj, :], in_=acc[:])
+            if jj == CHUNKS[c] - 1:
+                nc.sync.dma_start(out=out_v[:, starts[c] : starts[c] + CHUNKS[c], :], in_=osbs[c][:])
+
+        zs[0] = pro_a(0)
+        zs[1] = pro_a(1)
+        mbs[0] = pro_b(0, zs[0])
+        mbs[1] = pro_b(1, zs[1])
+        rules_regroup()
+        tabs[0] = pro_c(0, mbs[0])
+
+        for s in range(NT + 2):
+            if s == 2:
+                rules_quant()
+            if 0 <= s - 2 < NT:
+                quant(s - 2)
+            if s == 1:
+                tabs[1] = pro_c(1, mbs[1])
+            if s < NT:
+                c = chunk_of[s]
+                if c >= 1 and c + 1 < n_chunks:
+                    if s == starts[c] + 1:
+                        zs[c + 1] = pro_a(c + 1)
+                    if s == starts[c] + 3:
+                        tabs[c + 1] = pro_c(c + 1, mbs[c + 1])
+                gen(s)
+            if 0 <= s - 1 < NT:
+                trans(s - 1)
+            if 0 <= s - 2 < NT:
+                mx(s - 2)
+            if s < NT:
+                c = chunk_of[s]
+                if c >= 1 and c + 1 < n_chunks and s == starts[c] + 1:
+                    mbs[c + 1] = pro_b(c + 1, zs[c + 1])

@@ -5,6 +5,7 @@ from concourse.masks import make_identity
 
 F32 = mybir.dt.float32
 BF16 = mybir.dt.bfloat16
+I32 = mybir.dt.int32
 U32 = mybir.dt.uint32
 U8 = mybir.dt.uint8
 FP8X4 = mybir.dt.float8_e4m3fn_x4
@@ -17,16 +18,18 @@ B, I, M, O = 8192, 6, 4, 128
 R = M ** I
 NT = B // P
 CHUNKS = (2, 6, 8, 8, 8, 8, 8, 8, 8)
+STORES = (8, 8, 8, 8, 8, 8, 8, 4, 2, 1, 1)
 PASSES = R // 512
+NMOV = 256
 EPS = 1e-6
 FLOPS = 2 * B * R * O
 
 
 def scalar_share(j):
-    if j == 0:
+    if j < 3:
         return ()
     if j % 2 == 0:
-        return (5, 10, 15)
+        return (7, 11, 15)
     return (3, 7, 11, 15)
 
 
@@ -37,6 +40,10 @@ def tile_extendedanfis_kernel(tc, x, mfs, rules, out):
     chunk_of = []
     for c in range(n_chunks):
         chunk_of.extend([c] * CHUNKS[c])
+    st_starts = [sum(STORES[:c]) for c in range(len(STORES))]
+    store_of = []
+    for c in range(len(STORES)):
+        store_of.extend([c] * STORES[c])
     with ExitStack() as ctx:
         ctx.enter_context(tc.manual_schedule())
         const = ctx.enter_context(tc.tile_pool(name="const", bufs=1))
@@ -72,6 +79,25 @@ def tile_extendedanfis_kernel(tc, x, mfs, rules, out):
 
         out_v = out.rearrange("(p j) o -> p j o", j=NT)
 
+        rgrp = const.tile([P, PASSES, O, 4], BF16, align_bytes=64)
+        rwid = PASSES * O + NMOV - O
+        rcodes = const.tile([P, rwid], U32, align_bytes=64)
+        rscl = const.tile([P, rwid], U8, align_bytes=64)
+        if NMOV > O:
+            nc.vector.memset(rcodes[:, PASSES * O :].bitcast(I32), 0)
+            nc.vector.memset(rscl[:, PASSES * O :].bitcast(I32), 0)
+
+        def rules_regroup():
+            for g in range(0, PASSES, 2):
+                nc.scalar.copy(out=rgrp[:, g : g + 2, :, :], in_=rraw[:, g : g + 2, :, :].rearrange("p g t o -> p g o t"))
+
+        def rules_quant():
+            nc.vector.quantize_mx(
+                out=rcodes[:, : PASSES * O].bitcast(FP8X4),
+                scales=rscl[:, : PASSES * O],
+                in_=rgrp[:].rearrange("p g o t -> p (g o t)"),
+            )
+
         def pro_a(c):
             j0 = starts[c]
             nj = CHUNKS[c]
@@ -92,163 +118,196 @@ def tile_extendedanfis_kernel(tc, x, mfs, rules, out):
             nc.scalar.activation(out=mb[:], in_=z[:], func=ACT.Exp, scale=-0.5)
             return mb
 
+        def mul(dst, a, b):
+            return lambda: nc.vector.tensor_tensor(out=dst, in0=a, in1=b, op=ALU.mult)
+
         def pro_c(c, mb):
             nj = CHUNKS[c]
             ssum = pro.tile([P, nj, I], F32, tag="ssum")
-            nc.vector.tensor_reduce(out=ssum[:], in_=mb[:], axis=AX.X, op=ALU.add)
             t3 = pro.tile([P, nj, 3], F32, tag="t3")
-            nc.vector.tensor_tensor(out=t3[:], in0=ssum[:, :, 0:3], in1=ssum[:, :, 3:6], op=ALU.mult)
             den = pro.tile([P, nj, 1], F32, tag="den")
-            nc.vector.tensor_tensor(out=den[:], in0=t3[:, :, 0:1], in1=t3[:, :, 1:2], op=ALU.mult)
-            nc.vector.tensor_tensor(out=den[:], in0=den[:], in1=t3[:, :, 2:3], op=ALU.mult)
-            nc.vector.tensor_scalar_add(out=den[:], in0=den[:], scalar1=EPS)
             rn = pro.tile([P, nj, 1], F32, tag="rn")
-            nc.vector.reciprocal(out=rn[:], in_=den[:])
             m0n = pro.tile([P, nj, M], F32, tag="m0n")
-            nc.vector.tensor_tensor(out=m0n[:], in0=mb[:, :, 0, :], in1=rn[:].to_broadcast([P, nj, M]), op=ALU.mult)
             sq = [P, nj, M, M]
             s16 = tab.tile(sq, F32, tag="s16")
-            nc.vector.tensor_tensor(
-                out=s16[:],
-                in0=m0n[:].unsqueeze(3).to_broadcast(sq),
-                in1=mb[:, :, 1, :].unsqueeze(2).to_broadcast(sq),
-                op=ALU.mult,
-            )
             p23 = pro.tile(sq, F32, tag="p23")
-            nc.vector.tensor_tensor(
-                out=p23[:],
-                in0=mb[:, :, 2, :].unsqueeze(3).to_broadcast(sq),
-                in1=mb[:, :, 3, :].unsqueeze(2).to_broadcast(sq),
-                op=ALU.mult,
-            )
             p45 = pro.tile([P, nj, 2, M, 2], F32, tag="p45")
             r4 = tab.tile([P, nj, 2, 16, 8], F32, tag="r4")
+            ops = [
+                lambda: nc.vector.tensor_reduce(out=ssum[:], in_=mb[:], axis=AX.X, op=ALU.add),
+                mul(t3[:], ssum[:, :, 0:3], ssum[:, :, 3:6]),
+                mul(den[:], t3[:, :, 0:1], t3[:, :, 1:2]),
+                mul(den[:], den[:], t3[:, :, 2:3]),
+                lambda: nc.vector.tensor_scalar_add(out=den[:], in0=den[:], scalar1=EPS),
+                lambda: nc.vector.reciprocal(out=rn[:], in_=den[:]),
+                mul(m0n[:], mb[:, :, 0, :], rn[:].to_broadcast([P, nj, M])),
+                mul(s16[:], m0n[:].unsqueeze(3).to_broadcast(sq), mb[:, :, 1, :].unsqueeze(2).to_broadcast(sq)),
+                mul(p23[:], mb[:, :, 2, :].unsqueeze(3).to_broadcast(sq), mb[:, :, 3, :].unsqueeze(2).to_broadcast(sq)),
+            ]
             for u in range(2):
-                nc.vector.tensor_tensor(
-                    out=p45[:, :, u, :, :],
-                    in0=mb[:, :, 4, :].unsqueeze(3).to_broadcast([P, nj, M, 2]),
-                    in1=mb[:, :, 5, 2 * u : 2 * u + 2].unsqueeze(2).to_broadcast([P, nj, M, 2]),
-                    op=ALU.mult,
+                ops.append(
+                    mul(
+                        p45[:, :, u, :, :],
+                        mb[:, :, 4, :].unsqueeze(3).to_broadcast([P, nj, M, 2]),
+                        mb[:, :, 5, 2 * u : 2 * u + 2].unsqueeze(2).to_broadcast([P, nj, M, 2]),
+                    )
                 )
-            for u in range(2):
-                nc.vector.tensor_tensor(
-                    out=r4[:, :, u, :, :],
-                    in0=p23[:].rearrange("p j a b -> p j (a b)").unsqueeze(3).to_broadcast([P, nj, 16, 8]),
-                    in1=p45[:, :, u, :, :].rearrange("p j a b -> p j (a b)").unsqueeze(2).to_broadcast([P, nj, 16, 8]),
-                    op=ALU.mult,
-                )
-            return s16, r4
-
-        rgrp = const.tile([P, PASSES, O, 4], BF16, align_bytes=64)
-        rcodes = const.tile([P, PASSES * O], U32, align_bytes=64)
-        rscl = const.tile([P, PASSES * O], U8, align_bytes=64)
-
-        def rules_regroup():
-            for g in range(0, PASSES, 2):
-                nc.scalar.copy(out=rgrp[:, g : g + 2, :, :], in_=rraw[:, g : g + 2, :, :].rearrange("p g t o -> p g o t"))
-
-        def rules_quant():
-            nc.vector.quantize_mx(
-                out=rcodes[:].bitcast(FP8X4), scales=rscl[:], in_=rgrp[:].rearrange("p g o t -> p (g o t)")
-            )
+            hj = nj // 2
+            for lo in (0, hj):
+                for u in range(2):
+                    ops.append(
+                        mul(
+                            r4[:, lo : lo + hj, u, :, :],
+                            p23[:, lo : lo + hj].rearrange("p j a b -> p j (a b)").unsqueeze(3).to_broadcast([P, hj, 16, 8]),
+                            p45[:, lo : lo + hj, u, :, :]
+                            .rearrange("p j a b -> p j (a b)")
+                            .unsqueeze(2)
+                            .to_broadcast([P, hj, 16, 8]),
+                        )
+                    )
+            tabs[c] = (s16, r4)
+            return ops
 
         tabs = {}
         zs = {}
         mbs = {}
         nbs = {}
+        xts = {}
         grps = {}
         qs = {}
+        accs = {}
         osbs = {}
 
-        def gen(j):
+        def ok(j):
+            return 0 <= j < NT
+
+        def nb_tile(j, q):
+            if (j, q) not in nbs:
+                nb = nbp.tile([P, 2, 2, 2, 128], BF16, tag="nb%d" % q)
+                nbs[(j, q)] = nb
+            return nbs[(j, q)]
+
+        def gen_one(j, h, on_scalar):
             c = chunk_of[j]
             s16, r4 = tabs[c]
             jj = j - starts[c]
-            share = scalar_share(j)
-            nb = nbp.tile([P, PASSES, 2, 2, 128], BF16, tag="nb")
+            nb = nb_tile(j, h // 4)
+            dst = nb[:, (h // 2) % 2, :, h % 2, :]
             src = r4[:, jj, :, :, :].rearrange("p u a c -> p u (a c)")
-            for h in range(16):
-                dst = nb[:, h // 2, :, h % 2, :]
-                sc = s16[:, jj, h // 4, h % 4 : h % 4 + 1]
-                if h in share:
-                    nc.scalar.activation(out=dst, in_=src, func=ACT.Copy, scale=sc)
-                else:
-                    nc.vector.tensor_scalar_mul(out=dst, in0=src, scalar1=sc)
-            nbs[j] = nb
+            sc = s16[:, jj, h // 4, h % 4 : h % 4 + 1]
+            if on_scalar:
+                nc.scalar.activation(out=dst, in_=src, func=ACT.Copy, scale=sc)
+            else:
+                nc.vector.tensor_scalar_mul(out=dst, in0=src, scalar1=sc)
 
-        def trans(j):
-            nbw = nbs[j][:].rearrange("p g u s c -> p (g u s c)").bitcast(F32)
-            grp = grpp.tile([P, PASSES * P * 4], BF16, tag="grp", align_bytes=64)
-            gw = grp[:].bitcast(F32).rearrange("p (g b u) -> p g b u", g=PASSES, u=2)
-            xts = []
-            for q in range(4):
+        def gen_v(j, q):
+            if ok(j):
+                for h in range(4 * q, 4 * q + 4):
+                    if h not in scalar_share(j):
+                        gen_one(j, h, False)
+
+        def gen_s(j, q):
+            if ok(j):
+                for h in range(4 * q, 4 * q + 4):
+                    if h in scalar_share(j):
+                        gen_one(j, h, True)
+
+        def trans(j, q):
+            if ok(j):
+                nbw = nbs[(j, q)][:].rearrange("p g u s c -> p (g u s c)").bitcast(F32)
                 xt = ps_t.tile([P, 4, P], F32, tag="xt")
                 for r in range(4):
-                    blk = 4 * q + r
-                    nc.tensor.transpose(xt[:, r, :], nbw[:, blk * P : (blk + 1) * P], ident[:])
-                xts.append(xt)
-            for q in range(4):
+                    nc.tensor.transpose(xt[:, r, :], nbw[:, r * P : (r + 1) * P], ident[:])
+                xts[(j, q)] = xt
+
+        def evac(j, q):
+            if ok(j):
+                if q == 0:
+                    grp = grpp.tile([P, PASSES * P * 4], BF16, tag="grp", align_bytes=64)
+                    grps[j] = grp
+                gw = grps[j][:].bitcast(F32).rearrange("p (g b u) -> p g b u", g=PASSES, u=2)
                 nc.scalar.copy(
-                    out=gw[:, 2 * q : 2 * q + 2, :, :], in_=xts[q][:].rearrange("p (g u) b -> p g b u", u=2)
+                    out=gw[:, 2 * q : 2 * q + 2, :, :], in_=xts[(j, q)][:].rearrange("p (g u) b -> p g b u", u=2)
                 )
-            grps[j] = grp
 
         def quant(j):
-            codes = qp.tile([P, PASSES * P], U32, tag="codes", align_bytes=64)
-            scl = qp.tile([P, PASSES * P], U8, tag="scl", align_bytes=64)
-            nc.vector.quantize_mx(out=codes[:].bitcast(FP8X4), scales=scl[:], in_=grps[j][:])
-            qs[j] = (codes, scl)
+            if ok(j):
+                codes = qp.tile([P, PASSES * P], U32, tag="codes", align_bytes=64)
+                scl = qp.tile([P, PASSES * P], U8, tag="scl", align_bytes=64)
+                nc.vector.quantize_mx(out=codes[:].bitcast(FP8X4), scales=scl[:], in_=grps[j][:])
+                qs[j] = (codes, scl)
 
-        def mx(j):
-            codes, scl = qs[j]
-            acc = ps_a.tile([P, O], F32, tag="acc")
-            for g in range(PASSES):
-                cols = slice(g * P, (g + 1) * P)
-                nc.tensor.matmul_mx(
-                    out=acc[:],
-                    lhsT=codes[:, cols].bitcast(FP8X4),
-                    lhsT_scale=scl[:, cols],
-                    rhs=rcodes[:, cols].bitcast(FP8X4),
-                    rhs_scale=rscl[:, cols],
-                    start=(g == 0),
-                    stop=(g == PASSES - 1),
-                )
-            c = chunk_of[j]
-            jj = j - starts[c]
-            if jj == 0:
-                osb = outp.tile([P, CHUNKS[c], O], F32, tag="osb")
-                osbs[c] = osb
-            nc.scalar.copy(out=osbs[c][:, jj, :], in_=acc[:])
-            if jj == CHUNKS[c] - 1:
-                nc.sync.dma_start(out=out_v[:, starts[c] : starts[c] + CHUNKS[c], :], in_=osbs[c][:])
+        def mx(j, part):
+            if ok(j):
+                codes, scl = qs[j]
+                if part == 0:
+                    acc = ps_a.tile([P, NMOV], F32, tag="acc")
+                    accs[j] = acc
+                acc = accs[j]
+                for g in range(part * PASSES // 2, (part + 1) * PASSES // 2):
+                    nc.tensor.matmul_mx(
+                        out=acc[:],
+                        lhsT=codes[:, g * P : (g + 1) * P].bitcast(FP8X4),
+                        lhsT_scale=scl[:, g * P : (g + 1) * P],
+                        rhs=rcodes[:, g * O : g * O + NMOV].bitcast(FP8X4),
+                        rhs_scale=rscl[:, g * O : g * O + NMOV],
+                        start=(g == 0),
+                        stop=(g == PASSES - 1),
+                    )
+
+        def outcopy(j):
+            if ok(j):
+                c = store_of[j]
+                jj = j - st_starts[c]
+                if jj == 0:
+                    osb = outp.tile([P, STORES[c], O], F32, tag="osb")
+                    osbs[c] = osb
+                nc.scalar.copy(out=osbs[c][:, jj, :], in_=accs[j][:, :O])
+                if jj == STORES[c] - 1:
+                    nc.sync.dma_start(out=out_v[:, st_starts[c] : st_starts[c] + STORES[c], :], in_=osbs[c][:])
 
         zs[0] = pro_a(0)
         zs[1] = pro_a(1)
         mbs[0] = pro_b(0, zs[0])
         mbs[1] = pro_b(1, zs[1])
         rules_regroup()
-        tabs[0] = pro_c(0, mbs[0])
+        for op in pro_c(0, mbs[0]):
+            op()
+        fill = pro_c(1, mbs[1])
+        rate = len(fill)
 
-        for s in range(NT + 2):
+        for s in range(NT + 4):
+            trans(s - 1, 3)
+            evac(s - 1, 1)
+            gen_v(s, 0)
+            mx(s - 3, 0)
+            gen_s(s + 1, 0)
+            evac(s - 1, 2)
+            gen_v(s, 1)
+            trans(s, 0)
             if s == 2:
                 rules_quant()
-            if 0 <= s - 2 < NT:
-                quant(s - 2)
-            if s == 1:
-                tabs[1] = pro_c(1, mbs[1])
-            if s < NT:
+            quant(s - 2)
+            gen_s(s + 1, 1)
+            evac(s - 1, 3)
+            gen_v(s, 2)
+            trans(s, 1)
+            mx(s - 3, 1)
+            gen_s(s + 1, 2)
+            evac(s, 0)
+            gen_v(s, 3)
+            trans(s, 2)
+            outcopy(s - 3)
+            gen_s(s + 1, 3)
+            for op in fill[:rate]:
+                op()
+            fill = fill[rate:]
+            if ok(s):
                 c = chunk_of[s]
                 if c >= 1 and c + 1 < n_chunks:
-                    if s == starts[c] + 1:
+                    if s == starts[c]:
                         zs[c + 1] = pro_a(c + 1)
-                    if s == starts[c] + 3:
-                        tabs[c + 1] = pro_c(c + 1, mbs[c + 1])
-                gen(s)
-            if 0 <= s - 1 < NT:
-                trans(s - 1)
-            if 0 <= s - 2 < NT:
-                mx(s - 2)
-            if s < NT:
-                c = chunk_of[s]
-                if c >= 1 and c + 1 < n_chunks and s == starts[c] + 1:
-                    mbs[c + 1] = pro_b(c + 1, zs[c + 1])
+                        mbs[c + 1] = pro_b(c + 1, zs[c + 1])
+                    if s == starts[c] + 1:
+                        fill = pro_c(c + 1, mbs[c + 1])
+                        rate = 5

@@ -22,15 +22,14 @@ STORES = (8, 8, 8, 8, 8, 8, 8, 4, 2, 1, 1)
 PASSES = R // 512
 NMOV = 256
 EPS = 1e-6
+EARLY = 8
 FLOPS = 2 * B * R * O
 
 
 def scalar_share(j):
     if j < 3:
         return ()
-    if j % 2 == 0:
-        return (7, 11, 15)
-    return (3, 7, 11, 15)
+    return (7, 15)
 
 
 def tile_extendedanfis_kernel(tc, x, mfs, rules, out):
@@ -98,28 +97,36 @@ def tile_extendedanfis_kernel(tc, x, mfs, rules, out):
                 in_=rgrp[:].rearrange("p g o t -> p (g o t)"),
             )
 
+        tabs = {}
+        zs = {}
+        mbs = {}
+
+        def mul(dst, a, b):
+            return lambda: nc.vector.tensor_tensor(out=dst, in0=a, in1=b, op=ALU.mult)
+
         def pro_a(c):
             j0 = starts[c]
             nj = CHUNKS[c]
             full = [P, nj, I, M]
             z = pro.tile(full, F32, tag="z")
-            nc.vector.tensor_tensor(
-                out=z[:],
-                in0=x_sb[:, j0 : j0 + nj, :].unsqueeze(3).to_broadcast(full),
-                in1=mu[:].unsqueeze(1).to_broadcast(full),
-                op=ALU.subtract,
-            )
-            nc.vector.tensor_tensor(out=z[:], in0=z[:], in1=rs[:].unsqueeze(1).to_broadcast(full), op=ALU.mult)
-            return z
+            zs[c] = z
+            return [
+                lambda: nc.vector.tensor_tensor(
+                    out=z[:],
+                    in0=x_sb[:, j0 : j0 + nj, :].unsqueeze(3).to_broadcast(full),
+                    in1=mu[:].unsqueeze(1).to_broadcast(full),
+                    op=ALU.subtract,
+                ),
+                mul(z[:], z[:], rs[:].unsqueeze(1).to_broadcast(full)),
+            ]
 
-        def pro_b(c, z):
+        def pro_b1(c):
+            nc.scalar.activation(out=zs[c][:], in_=zs[c][:], func=ACT.Square)
+
+        def pro_b2(c):
             mb = pro.tile([P, CHUNKS[c], I, M], F32, tag="mb")
-            nc.scalar.activation(out=z[:], in_=z[:], func=ACT.Square)
-            nc.scalar.activation(out=mb[:], in_=z[:], func=ACT.Exp, scale=-0.5)
-            return mb
-
-        def mul(dst, a, b):
-            return lambda: nc.vector.tensor_tensor(out=dst, in0=a, in1=b, op=ALU.mult)
+            nc.scalar.activation(out=mb[:], in_=zs[c][:], func=ACT.Exp, scale=-0.5)
+            mbs[c] = mb
 
         def pro_c(c, mb):
             nj = CHUNKS[c]
@@ -168,9 +175,6 @@ def tile_extendedanfis_kernel(tc, x, mfs, rules, out):
             tabs[c] = (s16, r4)
             return ops
 
-        tabs = {}
-        zs = {}
-        mbs = {}
         nbs = {}
         xts = {}
         grps = {}
@@ -266,48 +270,59 @@ def tile_extendedanfis_kernel(tc, x, mfs, rules, out):
                 if jj == STORES[c] - 1:
                     nc.sync.dma_start(out=out_v[:, st_starts[c] : st_starts[c] + STORES[c], :], in_=osbs[c][:])
 
-        zs[0] = pro_a(0)
-        zs[1] = pro_a(1)
-        mbs[0] = pro_b(0, zs[0])
-        mbs[1] = pro_b(1, zs[1])
+        fill = []
+
+        def pop(n):
+            for op in fill[:n]:
+                op()
+            fill[:n] = []
+
+        for op in pro_a(0) + pro_a(1):
+            op()
+        pro_b1(0)
+        pro_b2(0)
+        pro_b1(1)
+        pro_b2(1)
         rules_regroup()
         for op in pro_c(0, mbs[0]):
             op()
-        fill = pro_c(1, mbs[1])
-        rate = len(fill)
+        fill.extend(pro_c(1, mbs[1]))
 
         for s in range(NT + 4):
+            n_pop = 2 if s < EARLY else 1
+            c = chunk_of[s] if ok(s) else 0
+            nxt = c >= 1 and c + 1 < n_chunks
+            if nxt and s == starts[c]:
+                assert len(fill) == 0
+                fill.extend(pro_a(c + 1))
             trans(s - 1, 3)
             evac(s - 1, 1)
             gen_v(s, 0)
+            pop(n_pop)
             mx(s - 3, 0)
             gen_s(s + 1, 0)
             evac(s - 1, 2)
             gen_v(s, 1)
+            pop(n_pop)
             trans(s, 0)
             if s == 2:
                 rules_quant()
             quant(s - 2)
             gen_s(s + 1, 1)
+            if nxt and s == starts[c]:
+                pro_b1(c + 1)
             evac(s - 1, 3)
             gen_v(s, 2)
+            pop(n_pop)
             trans(s, 1)
             mx(s - 3, 1)
             gen_s(s + 1, 2)
             evac(s, 0)
             gen_v(s, 3)
+            pop(n_pop)
             trans(s, 2)
             outcopy(s - 3)
             gen_s(s + 1, 3)
-            for op in fill[:rate]:
-                op()
-            fill = fill[rate:]
-            if ok(s):
-                c = chunk_of[s]
-                if c >= 1 and c + 1 < n_chunks:
-                    if s == starts[c]:
-                        zs[c + 1] = pro_a(c + 1)
-                        mbs[c + 1] = pro_b(c + 1, zs[c + 1])
-                    if s == starts[c] + 1:
-                        fill = pro_c(c + 1, mbs[c + 1])
-                        rate = 5
+            if nxt and s == starts[c]:
+                pro_b2(c + 1)
+                fill.extend(pro_c(c + 1, mbs[c + 1]))

@@ -29,7 +29,9 @@ FLOPS = 2 * B * R * O
 def scalar_share(j):
     if j < 3:
         return ()
-    return (7, 15)
+    if j % 2 == 0:
+        return (7, 11, 15)
+    return (3, 7, 11, 15)
 
 
 def tile_extendedanfis_kernel(tc, x, mfs, rules, out):
@@ -46,11 +48,11 @@ def tile_extendedanfis_kernel(tc, x, mfs, rules, out):
     with ExitStack() as ctx:
         ctx.enter_context(tc.manual_schedule())
         const = ctx.enter_context(tc.tile_pool(name="const", bufs=1))
-        pro = ctx.enter_context(tc.tile_pool(name="pro", bufs=2))
+        pro = ctx.enter_context(tc.tile_pool(name="pro", bufs=3))
         tab = ctx.enter_context(tc.tile_pool(name="tab", bufs=2))
-        nbp = ctx.enter_context(tc.tile_pool(name="nbp", bufs=3))
-        grpp = ctx.enter_context(tc.tile_pool(name="grpp", bufs=3))
-        qp = ctx.enter_context(tc.tile_pool(name="qp", bufs=3))
+        nbp = ctx.enter_context(tc.tile_pool(name="nbp", bufs=4))
+        grpp = ctx.enter_context(tc.tile_pool(name="grpp", bufs=4))
+        qp = ctx.enter_context(tc.tile_pool(name="qp", bufs=4))
         outp = ctx.enter_context(tc.tile_pool(name="outp", bufs=2))
         ps_t = ctx.enter_context(tc.psum_pool(name="ps_t", bufs=6))
         ps_a = ctx.enter_context(tc.psum_pool(name="ps_a", bufs=2))
@@ -277,52 +279,60 @@ def tile_extendedanfis_kernel(tc, x, mfs, rules, out):
                 op()
             fill[:n] = []
 
-        for op in pro_a(0) + pro_a(1):
+        for op in pro_a(0) + pro_a(1) + pro_a(2):
             op()
-        pro_b1(0)
-        pro_b2(0)
-        pro_b1(1)
-        pro_b2(1)
+        for c in range(3):
+            pro_b1(c)
+            pro_b2(c)
         rules_regroup()
         for op in pro_c(0, mbs[0]):
             op()
         fill.extend(pro_c(1, mbs[1]))
 
-        for s in range(NT + 4):
+        a_step = {}
+        c_step = {starts[1]: 2}
+        for c in range(3, n_chunks):
+            a_step[starts[c - 1] - 4] = c
+            c_step[starts[c - 1]] = c
+
+        for s in range(NT + 7):
             n_pop = 2 if s < EARLY else 1
-            c = chunk_of[s] if ok(s) else 0
-            nxt = c >= 1 and c + 1 < n_chunks
-            if nxt and s == starts[c]:
+            if s in a_step:
                 assert len(fill) == 0
-                fill.extend(pro_a(c + 1))
-            trans(s - 1, 3)
-            evac(s - 1, 1)
+                fill.extend(pro_a(a_step[s]))
+            if s in c_step:
+                assert len(fill) == 0
+                fill.extend(pro_c(c_step[s], mbs[c_step[s]]))
+            evac(s - 2, 1)
+            trans(s - 1, 0)
             gen_v(s, 0)
             pop(n_pop)
-            mx(s - 3, 0)
             gen_s(s + 1, 0)
-            evac(s - 1, 2)
+            outcopy(s - 6)
+
+            evac(s - 2, 2)
+            trans(s - 1, 1)
+            mx(s - 5, 0)
             gen_v(s, 1)
             pop(n_pop)
-            trans(s, 0)
+            gen_s(s + 1, 1)
+            if s - 2 in a_step:
+                pro_b1(a_step[s - 2])
             if s == 2:
                 rules_quant()
-            quant(s - 2)
-            gen_s(s + 1, 1)
-            if nxt and s == starts[c]:
-                pro_b1(c + 1)
-            evac(s - 1, 3)
+            quant(s - 3)
+
+            evac(s - 2, 3)
+            trans(s - 1, 2)
             gen_v(s, 2)
             pop(n_pop)
-            trans(s, 1)
-            mx(s - 3, 1)
             gen_s(s + 1, 2)
-            evac(s, 0)
+
+            evac(s - 1, 0)
+            trans(s - 1, 3)
+            mx(s - 5, 1)
             gen_v(s, 3)
             pop(n_pop)
-            trans(s, 2)
-            outcopy(s - 3)
             gen_s(s + 1, 3)
-            if nxt and s == starts[c]:
-                pro_b2(c + 1)
-                fill.extend(pro_c(c + 1, mbs[c + 1]))
+            if s - 2 in a_step:
+                pro_b2(a_step[s - 2])

@@ -27,10 +27,8 @@ FLOPS = 2 * B * R * O
 
 
 def scalar_share(j):
-    if j < 3:
+    if j < 3 or j >= NT - 3:
         return ()
-    if j % 2 == 0:
-        return (7, 11, 15)
     return (3, 7, 11, 15)
 
 
@@ -175,7 +173,8 @@ def tile_extendedanfis_kernel(tc, x, mfs, rules, out):
                         )
                     )
             tabs[c] = (s16, r4)
-            return ops
+            order = (0, 8, 1, 9, 2, 10, 3, 11, 4, 12, 5, 13, 6, 14, 7)
+            return [ops[k] for k in order]
 
         nbs = {}
         xts = {}
@@ -240,7 +239,14 @@ def tile_extendedanfis_kernel(tc, x, mfs, rules, out):
             if ok(j):
                 codes = qp.tile([P, PASSES * P], U32, tag="codes", align_bytes=64)
                 scl = qp.tile([P, PASSES * P], U8, tag="scl", align_bytes=64)
-                nc.vector.quantize_mx(out=codes[:].bitcast(FP8X4), scales=scl[:], in_=grps[j][:])
+                pieces = 2 if j == NT - 1 else 1
+                wid = PASSES * P // pieces
+                for k in range(pieces):
+                    nc.vector.quantize_mx(
+                        out=codes[:, k * wid : (k + 1) * wid].bitcast(FP8X4),
+                        scales=scl[:, k * wid : (k + 1) * wid],
+                        in_=grps[j][:, 4 * k * wid : 4 * (k + 1) * wid],
+                    )
                 qs[j] = (codes, scl)
 
         def mx(j, part):

@@ -27,7 +27,7 @@ FLOPS = 2 * B * R * O
 
 
 def scalar_share(j):
-    if j < 3 or j >= NT - 3:
+    if j < 1 or j >= NT - 3:
         return ()
     return (3, 7, 11, 15)
 
@@ -86,9 +86,9 @@ def tile_extendedanfis_kernel(tc, x, mfs, rules, out):
             nc.vector.memset(rcodes[:, PASSES * O :].bitcast(I32), 0)
             nc.vector.memset(rscl[:, PASSES * O :].bitcast(I32), 0)
 
-        def rules_regroup():
-            for g in range(0, PASSES, 2):
-                nc.scalar.copy(out=rgrp[:, g : g + 2, :, :], in_=rraw[:, g : g + 2, :, :].rearrange("p g t o -> p g o t"))
+        def rules_regroup(k):
+            g = 2 * k
+            nc.scalar.copy(out=rgrp[:, g : g + 2, :, :], in_=rraw[:, g : g + 2, :, :].rearrange("p g t o -> p g o t"))
 
         def rules_quant():
             nc.vector.quantize_mx(
@@ -131,50 +131,45 @@ def tile_extendedanfis_kernel(tc, x, mfs, rules, out):
         def pro_c(c, mb):
             nj = CHUNKS[c]
             ssum = pro.tile([P, nj, I], F32, tag="ssum")
-            t3 = pro.tile([P, nj, 3], F32, tag="t3")
             den = pro.tile([P, nj, 1], F32, tag="den")
             rn = pro.tile([P, nj, 1], F32, tag="rn")
-            m0n = pro.tile([P, nj, M], F32, tag="m0n")
             sq = [P, nj, M, M]
             s16 = tab.tile(sq, F32, tag="s16")
             p23 = pro.tile(sq, F32, tag="p23")
             p45 = pro.tile([P, nj, 2, M, 2], F32, tag="p45")
             r4 = tab.tile([P, nj, 2, 16, 8], F32, tag="r4")
-            ops = [
-                lambda: nc.vector.tensor_reduce(out=ssum[:], in_=mb[:], axis=AX.X, op=ALU.add),
-                mul(t3[:], ssum[:, :, 0:3], ssum[:, :, 3:6]),
-                mul(den[:], t3[:, :, 0:1], t3[:, :, 1:2]),
-                mul(den[:], den[:], t3[:, :, 2:3]),
-                lambda: nc.vector.tensor_scalar_add(out=den[:], in0=den[:], scalar1=EPS),
-                lambda: nc.vector.reciprocal(out=rn[:], in_=den[:]),
-                mul(m0n[:], mb[:, :, 0, :], rn[:].to_broadcast([P, nj, M])),
-                mul(s16[:], m0n[:].unsqueeze(3).to_broadcast(sq), mb[:, :, 1, :].unsqueeze(2).to_broadcast(sq)),
-                mul(p23[:], mb[:, :, 2, :].unsqueeze(3).to_broadcast(sq), mb[:, :, 3, :].unsqueeze(2).to_broadcast(sq)),
-            ]
-            for u in range(2):
-                ops.append(
-                    mul(
-                        p45[:, :, u, :, :],
-                        mb[:, :, 4, :].unsqueeze(3).to_broadcast([P, nj, M, 2]),
-                        mb[:, :, 5, 2 * u : 2 * u + 2].unsqueeze(2).to_broadcast([P, nj, M, 2]),
-                    )
+            s16f = s16[:].rearrange("p j a b -> p j (a b)")
+
+            def p45_part(u):
+                shp = [P, nj, M, 2]
+                return mul(
+                    p45[:, :, u, :, :],
+                    mb[:, :, 4, :].unsqueeze(3).to_broadcast(shp),
+                    mb[:, :, 5, 2 * u : 2 * u + 2].unsqueeze(2).to_broadcast(shp),
                 )
-            hj = nj // 2
-            for lo in (0, hj):
-                for u in range(2):
-                    ops.append(
-                        mul(
-                            r4[:, lo : lo + hj, u, :, :],
-                            p23[:, lo : lo + hj].rearrange("p j a b -> p j (a b)").unsqueeze(3).to_broadcast([P, hj, 16, 8]),
-                            p45[:, lo : lo + hj, u, :, :]
-                            .rearrange("p j a b -> p j (a b)")
-                            .unsqueeze(2)
-                            .to_broadcast([P, hj, 16, 8]),
-                        )
-                    )
+
+            def r4_part(u):
+                shp = [P, nj, 16, 8]
+                return mul(
+                    r4[:, :, u, :, :],
+                    p23[:].rearrange("p j a b -> p j (a b)").unsqueeze(3).to_broadcast(shp),
+                    p45[:, :, u, :, :].rearrange("p j a b -> p j (a b)").unsqueeze(2).to_broadcast(shp),
+                )
+
             tabs[c] = (s16, r4)
-            order = (0, 8, 1, 9, 2, 10, 3, 11, 4, 12, 5, 13, 6, 14, 7)
-            return [ops[k] for k in order]
+            return [
+                lambda: nc.vector.tensor_reduce(out=ssum[:], in_=mb[:], axis=AX.X, op=ALU.add),
+                mul(p23[:], mb[:, :, 2, :].unsqueeze(3).to_broadcast(sq), mb[:, :, 3, :].unsqueeze(2).to_broadcast(sq)),
+                lambda: nc.vector.tensor_reduce(out=den[:], in_=ssum[:], axis=AX.X, op=ALU.mult),
+                p45_part(0),
+                lambda: nc.vector.tensor_scalar_add(out=den[:], in0=den[:], scalar1=EPS),
+                p45_part(1),
+                lambda: nc.vector.reciprocal(out=rn[:], in_=den[:]),
+                mul(s16[:], mb[:, :, 0, :].unsqueeze(3).to_broadcast(sq), mb[:, :, 1, :].unsqueeze(2).to_broadcast(sq)),
+                r4_part(0),
+                mul(s16f, s16f, rn[:].to_broadcast([P, nj, M * M])),
+                r4_part(1),
+            ]
 
         nbs = {}
         xts = {}
@@ -290,7 +285,7 @@ def tile_extendedanfis_kernel(tc, x, mfs, rules, out):
         for c in range(3):
             pro_b1(c)
             pro_b2(c)
-        rules_regroup()
+        rules_regroup(0)
         for op in pro_c(0, mbs[0]):
             op()
         fill.extend(pro_c(1, mbs[1]))
@@ -302,7 +297,7 @@ def tile_extendedanfis_kernel(tc, x, mfs, rules, out):
             c_step[starts[c - 1]] = c
 
         for s in range(NT + 7):
-            n_pop = 2 if s < EARLY else 1
+            n_pop = 3 if s < 2 else (2 if s < EARLY else 1)
             if s in a_step:
                 assert len(fill) == 0
                 fill.extend(pro_a(a_step[s]))
@@ -324,7 +319,7 @@ def tile_extendedanfis_kernel(tc, x, mfs, rules, out):
             gen_s(s + 1, 1)
             if s - 2 in a_step:
                 pro_b1(a_step[s - 2])
-            if s == 2:
+            if s == 4:
                 rules_quant()
             quant(s - 3)
 
@@ -342,3 +337,5 @@ def tile_extendedanfis_kernel(tc, x, mfs, rules, out):
             gen_s(s + 1, 3)
             if s - 2 in a_step:
                 pro_b2(a_step[s - 2])
+            if s < 3:
+                rules_regroup(s + 1)

@@ -20,7 +20,7 @@ NT = B // P
 CHUNKS = (2, 6, 8, 8, 8, 8, 8, 8, 8)
 STORES = (8, 8, 8, 8, 8, 8, 8, 4, 2, 1, 1)
 PASSES = R // 512
-NMOV = 256
+NMOV = 128
 EPS = 1e-6
 EARLY = 8
 FLOPS = 2 * B * R * O

@@ -5,7 +5,6 @@ from concourse.masks import make_identity
 
 F32 = mybir.dt.float32
 BF16 = mybir.dt.bfloat16
-I32 = mybir.dt.int32
 U32 = mybir.dt.uint32
 U8 = mybir.dt.uint8
 FP8X4 = mybir.dt.float8_e4m3fn_x4
@@ -17,49 +16,52 @@ P = 128
 B, I, M, O = 8192, 6, 4, 128
 R = M ** I
 NT = B // P
-CHUNKS = (2, 6, 8, 8, 8, 8, 8, 8, 8)
-STORES = (8, 8, 8, 8, 8, 8, 8, 4, 2, 1, 1)
+IM = I * M
+GT = 4
+NG = NT // GT
+S16 = M * M
+SM = S16 + IM
+R4 = M ** 4
+CHUNKS = (4, 12, 12, 12, 12, 12)
+ACCS = (4,) * 15 + (2, 1, 1)
 PASSES = R // 512
-NMOV = 128
 EPS = 1e-6
-EARLY = 8
 FLOPS = 2 * B * R * O
 
 
 def scalar_share(j):
     if j < 1 or j >= NT - 3:
         return ()
-    return (3, 7, 11, 15)
+    return (3, 7, 15) if j % 2 else (7, 15)
 
 
 def tile_extendedanfis_kernel(tc, x, mfs, rules, out):
     nc = tc.nc
-    n_chunks = len(CHUNKS)
-    starts = [sum(CHUNKS[:c]) for c in range(n_chunks)]
+    starts = [sum(CHUNKS[:c]) for c in range(len(CHUNKS))]
     chunk_of = []
-    for c in range(n_chunks):
+    for c in range(len(CHUNKS)):
         chunk_of.extend([c] * CHUNKS[c])
-    st_starts = [sum(STORES[:c]) for c in range(len(STORES))]
-    store_of = []
-    for c in range(len(STORES)):
-        store_of.extend([c] * STORES[c])
+    acc_starts = [sum(ACCS[:c]) for c in range(len(ACCS))]
+    acc_of = []
+    for c in range(len(ACCS)):
+        acc_of.extend([c] * ACCS[c])
     with ExitStack() as ctx:
         ctx.enter_context(tc.manual_schedule())
         const = ctx.enter_context(tc.tile_pool(name="const", bufs=1))
-        pro = ctx.enter_context(tc.tile_pool(name="pro", bufs=3))
-        tab = ctx.enter_context(tc.tile_pool(name="tab", bufs=2))
+        tab = ctx.enter_context(tc.tile_pool(name="tab", bufs=3))
         nbp = ctx.enter_context(tc.tile_pool(name="nbp", bufs=4))
         grpp = ctx.enter_context(tc.tile_pool(name="grpp", bufs=4))
         qp = ctx.enter_context(tc.tile_pool(name="qp", bufs=4))
-        outp = ctx.enter_context(tc.tile_pool(name="outp", bufs=2))
-        ps_t = ctx.enter_context(tc.psum_pool(name="ps_t", bufs=6))
+        outp = ctx.enter_context(tc.tile_pool(name="outp", bufs=3))
+        ps_t = ctx.enter_context(tc.psum_pool(name="ps_t", bufs=4))
         ps_a = ctx.enter_context(tc.psum_pool(name="ps_a", bufs=2))
+        ps_q = ctx.enter_context(tc.psum_pool(name="ps_q", bufs=2))
 
         x_sb = const.tile([P, NT, I], BF16)
         nc.sync.dma_start(out=x_sb[:], in_=x.rearrange("(p j) i -> p j i", j=NT))
-        mfb = const.tile([P, I, M, 2], BF16)
+        mfb = const.tile([P, IM, 2], BF16)
         nc.scalar.dma_start(
-            out=mfb[:].rearrange("p i m c -> p (i m c)"),
+            out=mfb[:].rearrange("p f c -> p (f c)"),
             in_=mfs.rearrange("i m c -> (i m c)").partition_broadcast(P),
         )
         rraw = const.tile([P, PASSES, 4, O], BF16)
@@ -67,116 +69,197 @@ def tile_extendedanfis_kernel(tc, x, mfs, rules, out):
 
         ident = const.tile([P, P], F32)
         make_identity(nc, ident[:])
+        xrep = const.tile([P, NG, P], BF16, align_bytes=64)
+        nc.gpsimd.memset(xrep[:, :, GT * IM :], 0.0)
+        identb = const.tile([P, P], BF16, align_bytes=64)
+        nc.vector.tensor_copy(out=identb[:], in_=ident[:])
 
-        mu = const.tile([P, I, M], F32)
-        nc.vector.tensor_copy(out=mu[:], in_=mfb[:, :, :, 0])
-        sg = const.tile([P, I, M], F32)
-        nc.scalar.activation(out=sg[:], in_=mfb[:, :, :, 1], func=ACT.Abs)
-        nc.vector.tensor_scalar_add(out=sg[:], in0=sg[:], scalar1=EPS)
-        rs = const.tile([P, I, M], F32)
-        nc.vector.reciprocal(out=rs[:], in_=sg[:])
+        row = ident[:, : GT * IM].rearrange("p (j i m) -> p j i m", j=GT, i=I)
+        sq = [P, GT, M, M]
+        sels = const.tile([P, GT, SM], F32)
+        a23 = const.tile(sq, F32)
+        a45 = const.tile([P, GT, 2, M, 2], F32)
+        selr = const.tile([P, GT, 2, 16, 8], F32)
+
+        def add(eng, dst, a, b):
+            eng.tensor_tensor(out=dst, in0=a, in1=b, op=ALU.add)
+
+        add(nc.vector, a23[:], row[:, :, 2, :].unsqueeze(3).to_broadcast(sq), row[:, :, 3, :].unsqueeze(2).to_broadcast(sq))
+        for u in range(2):
+            shp = [P, GT, M, 2]
+            add(
+                nc.vector,
+                a45[:, :, u, :, :],
+                row[:, :, 4, :].unsqueeze(3).to_broadcast(shp),
+                row[:, :, 5, 2 * u : 2 * u + 2].unsqueeze(2).to_broadcast(shp),
+            )
+        add(
+            nc.gpsimd,
+            sels[:, :, :S16].rearrange("p j (a b) -> p j a b", a=M),
+            row[:, :, 0, :].unsqueeze(3).to_broadcast(sq),
+            row[:, :, 1, :].unsqueeze(2).to_broadcast(sq),
+        )
+        nc.gpsimd.tensor_copy(out=sels[:, :, S16:], in_=ident[:, : GT * IM].rearrange("p (j f) -> p j f", j=GT))
+        for u in range(2):
+            shp = [P, GT, 16, 8]
+            add(
+                nc.vector if u == 0 else nc.gpsimd,
+                selr[:, :, u, :, :],
+                a23[:].rearrange("p j a b -> p j (a b)").unsqueeze(3).to_broadcast(shp),
+                a45[:, :, u, :, :].rearrange("p j a b -> p j (a b)").unsqueeze(2).to_broadcast(shp),
+            )
+
+        sg = const.tile([P, IM], F32)
+        rsb = const.tile([P, 2, IM], F32)
+        rsel = const.tile([P, 2, GT, IM], F32)
+        rows = const.tile([P, 2, 1], F32)
+
+        def row_constants():
+            nc.vector.scalar_tensor_tensor(
+                out=sg[:], in0=mfb[:, :, 1], scalar=-1.0, in1=mfb[:, :, 1], op0=ALU.mult, op1=ALU.max
+            )
+            nc.vector.tensor_scalar_add(out=sg[:], in0=sg[:], scalar1=EPS)
+            nc.vector.reciprocal(out=rsb[:, 0, :], in_=sg[:])
+            nc.vector.scalar_tensor_tensor(
+                out=rsb[:, 1, :], in0=mfb[:, :, 0], scalar=-1.0, in1=rsb[:, 0, :], op0=ALU.mult, op1=ALU.mult
+            )
+
+        def row_select():
+            shp = [P, 2, GT, IM]
+            nc.vector.tensor_tensor(
+                out=rsel[:],
+                in0=ident[:, : GT * IM].rearrange("p (j f) -> p j f", j=GT).unsqueeze(1).to_broadcast(shp),
+                in1=rsb[:].unsqueeze(2).to_broadcast(shp),
+                op=ALU.mult,
+            )
+            nc.vector.tensor_reduce(
+                out=rows[:, :, 0], in_=rsel[:].rearrange("p c j f -> p c (j f)"), axis=AX.X, op=ALU.add
+            )
 
         out_v = out.rearrange("(p j) o -> p j o", j=NT)
 
         rgrp = const.tile([P, PASSES, O, 4], BF16, align_bytes=64)
-        rwid = PASSES * O + NMOV - O
-        rcodes = const.tile([P, rwid], U32, align_bytes=64)
-        rscl = const.tile([P, rwid], U8, align_bytes=64)
-        if NMOV > O:
-            nc.vector.memset(rcodes[:, PASSES * O :].bitcast(I32), 0)
-            nc.vector.memset(rscl[:, PASSES * O :].bitcast(I32), 0)
+        rcodes = const.tile([P, PASSES * O], U32, align_bytes=64)
+        rscl = const.tile([P, PASSES * O], U8, align_bytes=64)
 
         def rules_regroup(k):
             g = 2 * k
-            nc.scalar.copy(out=rgrp[:, g : g + 2, :, :], in_=rraw[:, g : g + 2, :, :].rearrange("p g t o -> p g o t"))
+            nc.vector.tensor_copy(
+                out=rgrp[:, g : g + 2, :, :], in_=rraw[:, g : g + 2, :, :].rearrange("p g t o -> p g o t")
+            )
 
         def rules_quant():
             nc.vector.quantize_mx(
-                out=rcodes[:, : PASSES * O].bitcast(FP8X4),
-                scales=rscl[:, : PASSES * O],
-                in_=rgrp[:].rearrange("p g o t -> p (g o t)"),
+                out=rcodes[:].bitcast(FP8X4), scales=rscl[:], in_=rgrp[:].rearrange("p g o t -> p (g o t)")
             )
 
-        tabs = {}
-        zs = {}
-        mbs = {}
+        feat = const.tile([P, NG, P], F32)
 
-        def mul(dst, a, b):
-            return lambda: nc.vector.tensor_tensor(out=dst, in0=a, in1=b, op=ALU.mult)
+        def replicate(g0, g1):
+            n = g1 - g0
+            nc.vector.tensor_copy(
+                out=xrep[:, g0:g1, : GT * IM].rearrange("p g (f m) -> p g f m", m=M),
+                in_=x_sb[:, GT * g0 : GT * g1, :]
+                .rearrange("p (g j) i -> p g (j i)", j=GT)
+                .unsqueeze(3)
+                .to_broadcast([P, n, GT * I, M]),
+            )
 
-        def pro_a(c):
-            j0 = starts[c]
+        def xtrans(g0, g1, pool, tag):
+            n = g1 - g0
+            xq = pool.tile([P, n, P], BF16, tag=tag)
+            for g in range(g0, g1):
+                nc.tensor.transpose(xq[:, g - g0, :], xrep[:, g, :], identb[:])
+            return xq
+
+        def square(g0, g1, xq):
+            nc.scalar.activation(
+                out=feat[:, g0:g1, :], in_=xq[:], func=ACT.Square, scale=rows[:, 0, :], bias=rows[:, 1, :]
+            )
+
+        smq = {}
+        sms = {}
+        s16s = {}
+
+        def small_mm(c):
+            ng = CHUNKS[c] // GT
+            q = ps_q.tile([P, ng, GT * SM], F32, tag="q")
+            for k in range(ng):
+                nc.tensor.matmul(
+                    out=q[:, k, :],
+                    lhsT=feat[:, starts[c] // GT + k, :],
+                    rhs=sels[:].rearrange("p j k -> p (j k)"),
+                    start=True,
+                    stop=True,
+                )
+            smq[c] = q
+
+        def small_exp(c):
+            sm = tab.tile([P, CHUNKS[c], SM], F32, tag="sm")
+            nc.scalar.activation(
+                out=sm[:].rearrange("p j k -> p (j k)"),
+                in_=smq[c][:].rearrange("p g k -> p (g k)"),
+                func=ACT.Exp,
+                scale=-0.5,
+            )
+            sms[c] = sm
+
+        def small_chain(c):
             nj = CHUNKS[c]
-            full = [P, nj, I, M]
-            z = pro.tile(full, F32, tag="z")
-            zs[c] = z
+            sm = sms[c]
+            ssum = tab.tile([P, nj, I], F32, tag="ssum")
+            den = tab.tile([P, nj, 1], F32, tag="den")
+            rn = tab.tile([P, nj, 1], F32, tag="rn")
+            s16 = tab.tile([P, nj, S16], F32, tag="s16")
+            s16s[c] = s16
             return [
-                lambda: nc.vector.tensor_tensor(
-                    out=z[:],
-                    in0=x_sb[:, j0 : j0 + nj, :].unsqueeze(3).to_broadcast(full),
-                    in1=mu[:].unsqueeze(1).to_broadcast(full),
-                    op=ALU.subtract,
+                lambda: nc.vector.tensor_reduce(
+                    out=ssum[:], in_=sm[:, :, S16:].rearrange("p j (i m) -> p j i m", m=M), axis=AX.X, op=ALU.add
                 ),
-                mul(z[:], z[:], rs[:].unsqueeze(1).to_broadcast(full)),
-            ]
-
-        def pro_b1(c):
-            nc.scalar.activation(out=zs[c][:], in_=zs[c][:], func=ACT.Square)
-
-        def pro_b2(c):
-            mb = pro.tile([P, CHUNKS[c], I, M], F32, tag="mb")
-            nc.scalar.activation(out=mb[:], in_=zs[c][:], func=ACT.Exp, scale=-0.5)
-            mbs[c] = mb
-
-        def pro_c(c, mb):
-            nj = CHUNKS[c]
-            ssum = pro.tile([P, nj, I], F32, tag="ssum")
-            den = pro.tile([P, nj, 1], F32, tag="den")
-            rn = pro.tile([P, nj, 1], F32, tag="rn")
-            sq = [P, nj, M, M]
-            s16 = tab.tile(sq, F32, tag="s16")
-            p23 = pro.tile(sq, F32, tag="p23")
-            p45 = pro.tile([P, nj, 2, M, 2], F32, tag="p45")
-            r4 = tab.tile([P, nj, 2, 16, 8], F32, tag="r4")
-            s16f = s16[:].rearrange("p j a b -> p j (a b)")
-
-            def p45_part(u):
-                shp = [P, nj, M, 2]
-                return mul(
-                    p45[:, :, u, :, :],
-                    mb[:, :, 4, :].unsqueeze(3).to_broadcast(shp),
-                    mb[:, :, 5, 2 * u : 2 * u + 2].unsqueeze(2).to_broadcast(shp),
-                )
-
-            def r4_part(u):
-                shp = [P, nj, 16, 8]
-                return mul(
-                    r4[:, :, u, :, :],
-                    p23[:].rearrange("p j a b -> p j (a b)").unsqueeze(3).to_broadcast(shp),
-                    p45[:, :, u, :, :].rearrange("p j a b -> p j (a b)").unsqueeze(2).to_broadcast(shp),
-                )
-
-            tabs[c] = (s16, r4)
-            return [
-                lambda: nc.vector.tensor_reduce(out=ssum[:], in_=mb[:], axis=AX.X, op=ALU.add),
-                mul(p23[:], mb[:, :, 2, :].unsqueeze(3).to_broadcast(sq), mb[:, :, 3, :].unsqueeze(2).to_broadcast(sq)),
                 lambda: nc.vector.tensor_reduce(out=den[:], in_=ssum[:], axis=AX.X, op=ALU.mult),
-                p45_part(0),
                 lambda: nc.vector.tensor_scalar_add(out=den[:], in0=den[:], scalar1=EPS),
-                p45_part(1),
                 lambda: nc.vector.reciprocal(out=rn[:], in_=den[:]),
-                mul(s16[:], mb[:, :, 0, :].unsqueeze(3).to_broadcast(sq), mb[:, :, 1, :].unsqueeze(2).to_broadcast(sq)),
-                r4_part(0),
-                mul(s16f, s16f, rn[:].to_broadcast([P, nj, M * M])),
-                r4_part(1),
+                lambda: nc.vector.tensor_tensor(
+                    out=s16[:], in0=sm[:, :, :S16], in1=rn[:].to_broadcast([P, nj, S16]), op=ALU.mult
+                ),
             ]
+
+        r4q = {}
+        r4s = {}
+
+        def r4_mm(j, alone=False):
+            if j < NT:
+                if alone or j % 2 == 0:
+                    q = ps_q.tile([P, 1 if alone else 2, R4], F32, tag="q")
+                    r4q[j] = (q, 0)
+                else:
+                    r4q[j] = (r4q[j - 1][0], 1)
+                q, k = r4q[j]
+                nc.tensor.matmul(
+                    out=q[:, k, :],
+                    lhsT=feat[:, j // GT, :],
+                    rhs=selr[:, j % GT, :, :, :].rearrange("p u a c -> p (u a c)"),
+                    start=True,
+                    stop=True,
+                )
+
+        def r4_exp(j, n):
+            if j < NT:
+                if j % 2 == 0:
+                    r4 = tab.tile([P, 2, 2, 128], F32, tag="r4")
+                    r4s[j // 2] = r4
+                nc.scalar.activation(
+                    out=r4s[j // 2][:, j % 2 : j % 2 + n, :, :].rearrange("p j u c -> p (j u c)"),
+                    in_=r4q[j][0][:].rearrange("p j k -> p (j k)"),
+                    func=ACT.Exp,
+                    scale=-0.5,
+                )
 
         nbs = {}
         xts = {}
         grps = {}
         qs = {}
         accs = {}
-        osbs = {}
 
         def ok(j):
             return 0 <= j < NT
@@ -188,13 +271,11 @@ def tile_extendedanfis_kernel(tc, x, mfs, rules, out):
             return nbs[(j, q)]
 
         def gen_one(j, h, on_scalar):
-            c = chunk_of[j]
-            s16, r4 = tabs[c]
-            jj = j - starts[c]
             nb = nb_tile(j, h // 4)
             dst = nb[:, (h // 2) % 2, :, h % 2, :]
-            src = r4[:, jj, :, :, :].rearrange("p u a c -> p u (a c)")
-            sc = s16[:, jj, h // 4, h % 4 : h % 4 + 1]
+            src = r4s[j // 2][:, j % 2, :, :]
+            c = chunk_of[j]
+            sc = s16s[c][:, j - starts[c], h : h + 1]
             if on_scalar:
                 nc.scalar.activation(out=dst, in_=src, func=ACT.Copy, scale=sc)
             else:
@@ -247,31 +328,28 @@ def tile_extendedanfis_kernel(tc, x, mfs, rules, out):
         def mx(j, part):
             if ok(j):
                 codes, scl = qs[j]
-                if part == 0:
-                    acc = ps_a.tile([P, NMOV], F32, tag="acc")
-                    accs[j] = acc
-                acc = accs[j]
+                c = acc_of[j]
+                if j == acc_starts[c] and part == 0:
+                    acc = ps_a.tile([P, ACCS[c], O], F32, tag="acc")
+                    accs[c] = acc
                 for g in range(part * PASSES // 2, (part + 1) * PASSES // 2):
                     nc.tensor.matmul_mx(
-                        out=acc[:],
+                        out=accs[c][:, j - acc_starts[c], :],
                         lhsT=codes[:, g * P : (g + 1) * P].bitcast(FP8X4),
                         lhsT_scale=scl[:, g * P : (g + 1) * P],
-                        rhs=rcodes[:, g * O : g * O + NMOV].bitcast(FP8X4),
-                        rhs_scale=rscl[:, g * O : g * O + NMOV],
+                        rhs=rcodes[:, g * O : (g + 1) * O].bitcast(FP8X4),
+                        rhs_scale=rscl[:, g * O : (g + 1) * O],
                         start=(g == 0),
                         stop=(g == PASSES - 1),
                     )
 
         def outcopy(j):
             if ok(j):
-                c = store_of[j]
-                jj = j - st_starts[c]
-                if jj == 0:
-                    osb = outp.tile([P, STORES[c], O], F32, tag="osb")
-                    osbs[c] = osb
-                nc.scalar.copy(out=osbs[c][:, jj, :], in_=accs[j][:, :O])
-                if jj == STORES[c] - 1:
-                    nc.sync.dma_start(out=out_v[:, st_starts[c] : st_starts[c] + STORES[c], :], in_=osbs[c][:])
+                c = acc_of[j]
+                if j == acc_starts[c] + ACCS[c] - 1:
+                    osb = outp.tile([P, ACCS[c], O], F32, tag="osb")
+                    nc.scalar.copy(out=osb[:], in_=accs[c][:])
+                    nc.sync.dma_start(out=out_v[:, acc_starts[c] : acc_starts[c] + ACCS[c], :], in_=osb[:])
 
         fill = []
 
@@ -280,45 +358,58 @@ def tile_extendedanfis_kernel(tc, x, mfs, rules, out):
                 op()
             fill[:n] = []
 
-        for op in pro_a(0) + pro_a(1) + pro_a(2):
+        row_constants()
+        replicate(0, 1)
+        row_select()
+        xq0 = xtrans(0, 1, ps_q, "q")
+        square(0, 1, xq0)
+        small_mm(0)
+        small_exp(0)
+        r4_mm(0, alone=True)
+        r4_exp(0, 1)
+        replicate(1, NG)
+        r4_mm(1, alone=True)
+        r4_exp(1, 1)
+        xq1 = xtrans(1, 8, ps_t, "xt")
+        xq2 = xtrans(8, NG, ps_t, "xt")
+        square(1, 8, xq1)
+        square(8, NG, xq2)
+        for op in small_chain(0):
             op()
-        for c in range(3):
-            pro_b1(c)
-            pro_b2(c)
-        rules_regroup(0)
-        for op in pro_c(0, mbs[0]):
-            op()
-        fill.extend(pro_c(1, mbs[1]))
+        r4_mm(2)
+        r4_mm(3)
+        small_mm(1)
 
-        a_step = {}
-        c_step = {starts[1]: 2}
-        for c in range(3, n_chunks):
-            a_step[starts[c - 1] - 4] = c
-            c_step[starts[c - 1]] = c
+        mm_step = {}
+        exp_step = {}
+        chain_step = {1: 1}
+        exp_step[0] = 1
+        for c in range(2, len(CHUNKS)):
+            mm_step[starts[c] - 7] = c
+            exp_step[starts[c] - 5] = c
+            chain_step[starts[c] - 4] = c
 
         for s in range(NT + 7):
-            n_pop = 3 if s < 2 else (2 if s < EARLY else 1)
-            if s in a_step:
+            if s in chain_step:
                 assert len(fill) == 0
-                fill.extend(pro_a(a_step[s]))
-            if s in c_step:
-                assert len(fill) == 0
-                fill.extend(pro_c(c_step[s], mbs[c_step[s]]))
+                fill.extend(small_chain(chain_step[s]))
             evac(s - 2, 1)
             trans(s - 1, 0)
             gen_v(s, 0)
-            pop(n_pop)
+            pop(1)
             gen_s(s + 1, 0)
+            if s % 2 == 0:
+                r4_exp(s + 2, 2)
             outcopy(s - 6)
 
             evac(s - 2, 2)
             trans(s - 1, 1)
             mx(s - 5, 0)
             gen_v(s, 1)
-            pop(n_pop)
+            pop(1)
             gen_s(s + 1, 1)
-            if s - 2 in a_step:
-                pro_b1(a_step[s - 2])
+            if s in exp_step:
+                small_exp(exp_step[s])
             if s == 4:
                 rules_quant()
             quant(s - 3)
@@ -326,16 +417,17 @@ def tile_extendedanfis_kernel(tc, x, mfs, rules, out):
             evac(s - 2, 3)
             trans(s - 1, 2)
             gen_v(s, 2)
-            pop(n_pop)
+            pop(1)
             gen_s(s + 1, 2)
+            r4_mm(s + 4)
 
             evac(s - 1, 0)
             trans(s - 1, 3)
             mx(s - 5, 1)
             gen_v(s, 3)
-            pop(n_pop)
+            pop(1)
             gen_s(s + 1, 3)
-            if s - 2 in a_step:
-                pro_b2(a_step[s - 2])
-            if s < 3:
-                rules_regroup(s + 1)
+            if s in mm_step:
+                small_mm(mm_step[s])
+            if s < 4:
+                rules_regroup(s)

@@ -30,9 +30,9 @@ FLOPS = 2 * B * R * O
 
 
 def scalar_share(j):
-    if j < 1 or j >= NT - 3:
-        return ()
-    return (3, 7, 15) if j % 2 else (7, 15)
+    if j >= NT - 3:
+        return ((7, 15), (7,), ())[j - NT + 3]
+    return (3, 7, 11, 15) if j == 0 else ((3, 7, 15) if j % 3 else (7, 15))
 
 
 def tile_extendedanfis_kernel(tc, x, mfs, rules, out):
@@ -65,49 +65,47 @@ def tile_extendedanfis_kernel(tc, x, mfs, rules, out):
             in_=mfs.rearrange("i m c -> (i m c)").partition_broadcast(P),
         )
         rraw = const.tile([P, PASSES, 4, O], BF16)
-        nc.sync.dma_start(out=rraw[:], in_=rules.rearrange("(g p t) o -> p g t o", p=P, t=4))
+        rules_v = rules.rearrange("(z a y q w) o -> z y a q (w o)", z=M, y=M, q=8, w=2)
+        for z in range(M):
+            for y in range(M):
+                nc.sync.dma_start(
+                    out=rraw[:, 2 * z + y // 2, 2 * (y % 2) : 2 * (y % 2) + 2, :].rearrange("p w o -> p (w o)"),
+                    in_=rules_v[z, y],
+                )
 
+        xrep = const.tile([P, NG, P], BF16, align_bytes=64)
+        nc.vector.memset(xrep[:, :, GT * IM :], 0.0)
         ident = const.tile([P, P], F32)
         make_identity(nc, ident[:])
-        xrep = const.tile([P, NG, P], BF16, align_bytes=64)
-        nc.gpsimd.memset(xrep[:, :, GT * IM :], 0.0)
         identb = const.tile([P, P], BF16, align_bytes=64)
         nc.vector.tensor_copy(out=identb[:], in_=ident[:])
 
         row = ident[:, : GT * IM].rearrange("p (j i m) -> p j i m", j=GT, i=I)
         sq = [P, GT, M, M]
         sels = const.tile([P, GT, SM], F32)
-        a23 = const.tile(sq, F32)
-        a45 = const.tile([P, GT, 2, M, 2], F32)
-        selr = const.tile([P, GT, 2, 16, 8], F32)
+        a12 = const.tile(sq, F32)
+        a45 = const.tile(sq, F32)
+        selr = const.tile([P, GT, 16, 16], F32)
 
-        def add(eng, dst, a, b):
-            eng.tensor_tensor(out=dst, in0=a, in1=b, op=ALU.add)
+        def add(dst, a, b):
+            nc.vector.tensor_tensor(out=dst, in0=a, in1=b, op=ALU.add)
 
-        add(nc.vector, a23[:], row[:, :, 2, :].unsqueeze(3).to_broadcast(sq), row[:, :, 3, :].unsqueeze(2).to_broadcast(sq))
-        for u in range(2):
-            shp = [P, GT, M, 2]
+        def outer(dst, i, k):
+            add(dst, row[:, :, i, :].unsqueeze(3).to_broadcast(sq), row[:, :, k, :].unsqueeze(2).to_broadcast(sq))
+
+        def selr_part(j0):
+            shp = [P, 2, 16, 16]
             add(
-                nc.vector,
-                a45[:, :, u, :, :],
-                row[:, :, 4, :].unsqueeze(3).to_broadcast(shp),
-                row[:, :, 5, 2 * u : 2 * u + 2].unsqueeze(2).to_broadcast(shp),
+                selr[:, j0 : j0 + 2, :, :],
+                a12[:, j0 : j0 + 2, :, :].rearrange("p j a b -> p j (a b)").unsqueeze(3).to_broadcast(shp),
+                a45[:, j0 : j0 + 2, :, :].rearrange("p j a b -> p j (a b)").unsqueeze(2).to_broadcast(shp),
             )
-        add(
-            nc.gpsimd,
-            sels[:, :, :S16].rearrange("p j (a b) -> p j a b", a=M),
-            row[:, :, 0, :].unsqueeze(3).to_broadcast(sq),
-            row[:, :, 1, :].unsqueeze(2).to_broadcast(sq),
-        )
-        nc.gpsimd.tensor_copy(out=sels[:, :, S16:], in_=ident[:, : GT * IM].rearrange("p (j f) -> p j f", j=GT))
-        for u in range(2):
-            shp = [P, GT, 16, 8]
-            add(
-                nc.vector if u == 0 else nc.gpsimd,
-                selr[:, :, u, :, :],
-                a23[:].rearrange("p j a b -> p j (a b)").unsqueeze(3).to_broadcast(shp),
-                a45[:, :, u, :, :].rearrange("p j a b -> p j (a b)").unsqueeze(2).to_broadcast(shp),
-            )
+
+        outer(sels[:, :, :S16].rearrange("p j (a b) -> p j a b", a=M), 0, 3)
+        nc.vector.tensor_copy(out=sels[:, :, S16:], in_=ident[:, : GT * IM].rearrange("p (j f) -> p j f", j=GT))
+        outer(a12[:], 1, 2)
+        outer(a45[:], 4, 5)
+        selr_part(0)
 
         sg = const.tile([P, IM], F32)
         rsb = const.tile([P, 2, IM], F32)
@@ -144,7 +142,8 @@ def tile_extendedanfis_kernel(tc, x, mfs, rules, out):
 
         def rules_regroup(k):
             g = 2 * k
-            nc.vector.tensor_copy(
+            copy = nc.scalar.copy if k < 2 else nc.vector.tensor_copy
+            copy(
                 out=rgrp[:, g : g + 2, :, :], in_=rraw[:, g : g + 2, :, :].rearrange("p g t o -> p g o t")
             )
 
@@ -238,7 +237,7 @@ def tile_extendedanfis_kernel(tc, x, mfs, rules, out):
                 nc.tensor.matmul(
                     out=q[:, k, :],
                     lhsT=feat[:, j // GT, :],
-                    rhs=selr[:, j % GT, :, :, :].rearrange("p u a c -> p (u a c)"),
+                    rhs=selr[:, j % GT, :, :].rearrange("p a c -> p (a c)"),
                     start=True,
                     stop=True,
                 )
@@ -246,10 +245,10 @@ def tile_extendedanfis_kernel(tc, x, mfs, rules, out):
         def r4_exp(j, n):
             if j < NT:
                 if j % 2 == 0:
-                    r4 = tab.tile([P, 2, 2, 128], F32, tag="r4")
+                    r4 = tab.tile([P, 2, R4], F32, tag="r4")
                     r4s[j // 2] = r4
                 nc.scalar.activation(
-                    out=r4s[j // 2][:, j % 2 : j % 2 + n, :, :].rearrange("p j u c -> p (j u c)"),
+                    out=r4s[j // 2][:, j % 2 : j % 2 + n, :].rearrange("p j k -> p (j k)"),
                     in_=r4q[j][0][:].rearrange("p j k -> p (j k)"),
                     func=ACT.Exp,
                     scale=-0.5,
@@ -266,14 +265,14 @@ def tile_extendedanfis_kernel(tc, x, mfs, rules, out):
 
         def nb_tile(j, q):
             if (j, q) not in nbs:
-                nb = nbp.tile([P, 2, 2, 2, 128], BF16, tag="nb%d" % q)
+                nb = nbp.tile([P, 4, R4], BF16, tag="nb%d" % q)
                 nbs[(j, q)] = nb
             return nbs[(j, q)]
 
         def gen_one(j, h, on_scalar):
             nb = nb_tile(j, h // 4)
-            dst = nb[:, (h // 2) % 2, :, h % 2, :]
-            src = r4s[j // 2][:, j % 2, :, :]
+            dst = nb[:, h % 4, :]
+            src = r4s[j // 2][:, j % 2, :]
             c = chunk_of[j]
             sc = s16s[c][:, j - starts[c], h : h + 1]
             if on_scalar:
@@ -295,7 +294,7 @@ def tile_extendedanfis_kernel(tc, x, mfs, rules, out):
 
         def trans(j, q):
             if ok(j):
-                nbw = nbs[(j, q)][:].rearrange("p g u s c -> p (g u s c)").bitcast(F32)
+                nbw = nbs[(j, q)][:].rearrange("p h c -> p (h c)").bitcast(F32)
                 xt = ps_t.tile([P, 4, P], F32, tag="xt")
                 for r in range(4):
                     nc.tensor.transpose(xt[:, r, :], nbw[:, r * P : (r + 1) * P], ident[:])
@@ -358,9 +357,10 @@ def tile_extendedanfis_kernel(tc, x, mfs, rules, out):
                 op()
             fill[:n] = []
 
-        row_constants()
         replicate(0, 1)
+        row_constants()
         row_select()
+        selr_part(2)
         xq0 = xtrans(0, 1, ps_q, "q")
         square(0, 1, xq0)
         small_mm(0)
@@ -369,13 +369,15 @@ def tile_extendedanfis_kernel(tc, x, mfs, rules, out):
         r4_exp(0, 1)
         replicate(1, NG)
         r4_mm(1, alone=True)
+        for op in small_chain(0):
+            op()
+        for q in range(4):
+            gen_s(0, q)
         r4_exp(1, 1)
         xq1 = xtrans(1, 8, ps_t, "xt")
         xq2 = xtrans(8, NG, ps_t, "xt")
         square(1, 8, xq1)
         square(8, NG, xq2)
-        for op in small_chain(0):
-            op()
         r4_mm(2)
         r4_mm(3)
         small_mm(1)
@@ -408,6 +410,8 @@ def tile_extendedanfis_kernel(tc, x, mfs, rules, out):
             gen_v(s, 1)
             pop(1)
             gen_s(s + 1, 1)
+            if s == 1:
+                rules_regroup(0)
             if s in exp_step:
                 small_exp(exp_step[s])
             if s == 4:
@@ -429,5 +433,5 @@ def tile_extendedanfis_kernel(tc, x, mfs, rules, out):
             gen_s(s + 1, 3)
             if s in mm_step:
                 small_mm(mm_step[s])
-            if s < 4:
+            if s in (1, 2, 3):
                 rules_regroup(s)

@@ -32,7 +32,9 @@ FLOPS = 2 * B * R * O
 def scalar_share(j):
     if j >= NT - 3:
         return ((7, 15), (7,), ())[j - NT + 3]
-    return (3, 7, 11, 15) if j == 0 else ((3, 7, 15) if j % 3 else (7, 15))
+    if j == 0:
+        return (3, 7, 11, 15)
+    return (7, 15) if j % 3 else (3, 7, 15)
 
 
 def tile_extendedanfis_kernel(tc, x, mfs, rules, out):
@@ -140,9 +142,8 @@ def tile_extendedanfis_kernel(tc, x, mfs, rules, out):
         rcodes = const.tile([P, PASSES * O], U32, align_bytes=64)
         rscl = const.tile([P, PASSES * O], U8, align_bytes=64)
 
-        def rules_regroup(k):
+        def rules_regroup(k, copy):
             g = 2 * k
-            copy = nc.scalar.copy if k < 2 else nc.vector.tensor_copy
             copy(
                 out=rgrp[:, g : g + 2, :, :], in_=rraw[:, g : g + 2, :, :].rearrange("p g t o -> p g o t")
             )
@@ -363,29 +364,29 @@ def tile_extendedanfis_kernel(tc, x, mfs, rules, out):
         selr_part(2)
         xq0 = xtrans(0, 1, ps_q, "q")
         square(0, 1, xq0)
+        rules_regroup(0, nc.scalar.copy)
         small_mm(0)
         small_exp(0)
         r4_mm(0, alone=True)
         r4_exp(0, 1)
-        replicate(1, NG)
+        replicate(1, 4)
         r4_mm(1, alone=True)
         for op in small_chain(0):
             op()
         for q in range(4):
             gen_s(0, q)
         r4_exp(1, 1)
-        xq1 = xtrans(1, 8, ps_t, "xt")
-        xq2 = xtrans(8, NG, ps_t, "xt")
-        square(1, 8, xq1)
-        square(8, NG, xq2)
+        xq1 = xtrans(1, 4, ps_t, "xt")
+        square(1, 4, xq1)
         r4_mm(2)
         r4_mm(3)
         small_mm(1)
 
         mm_step = {}
         exp_step = {}
-        chain_step = {1: 1}
+        chain_step = {2: 1}
         exp_step[0] = 1
+        late = {0: (4, 10), 1: (10, NG)}
         for c in range(2, len(CHUNKS)):
             mm_step[starts[c] - 7] = c
             exp_step[starts[c] - 5] = c
@@ -398,7 +399,7 @@ def tile_extendedanfis_kernel(tc, x, mfs, rules, out):
             evac(s - 2, 1)
             trans(s - 1, 0)
             gen_v(s, 0)
-            pop(1)
+            pop(2 if s < 4 else 1)
             gen_s(s + 1, 0)
             if s % 2 == 0:
                 r4_exp(s + 2, 2)
@@ -408,10 +409,8 @@ def tile_extendedanfis_kernel(tc, x, mfs, rules, out):
             trans(s - 1, 1)
             mx(s - 5, 0)
             gen_v(s, 1)
-            pop(1)
+            pop(2 if s < 4 else 1)
             gen_s(s + 1, 1)
-            if s == 1:
-                rules_regroup(0)
             if s in exp_step:
                 small_exp(exp_step[s])
             if s == 4:
@@ -421,7 +420,7 @@ def tile_extendedanfis_kernel(tc, x, mfs, rules, out):
             evac(s - 2, 3)
             trans(s - 1, 2)
             gen_v(s, 2)
-            pop(1)
+            pop(2 if s < 4 else 1)
             gen_s(s + 1, 2)
             r4_mm(s + 4)
 
@@ -429,9 +428,13 @@ def tile_extendedanfis_kernel(tc, x, mfs, rules, out):
             trans(s - 1, 3)
             mx(s - 5, 1)
             gen_v(s, 3)
-            pop(1)
+            pop(2 if s < 4 else 1)
             gen_s(s + 1, 3)
             if s in mm_step:
                 small_mm(mm_step[s])
             if s in (1, 2, 3):
-                rules_regroup(s)
+                rules_regroup(s, nc.vector.tensor_copy)
+            if s in late:
+                g0, g1 = late[s]
+                replicate(g0, g1)
+                square(g0, g1, xtrans(g0, g1, ps_t, "xt"))

@@ -34,7 +34,7 @@ def scalar_share(j):
         return ((7, 15), (7,), ())[j - NT + 3]
     if j == 0:
         return (3, 7, 11, 15)
-    return (7, 15) if j % 3 else (3, 7, 15)
+    return (7, 15) if j % 2 else (3, 7, 15)
 
 
 def tile_extendedanfis_kernel(tc, x, mfs, rules, out):
@@ -54,7 +54,7 @@ def tile_extendedanfis_kernel(tc, x, mfs, rules, out):
         nbp = ctx.enter_context(tc.tile_pool(name="nbp", bufs=4))
         grpp = ctx.enter_context(tc.tile_pool(name="grpp", bufs=4))
         qp = ctx.enter_context(tc.tile_pool(name="qp", bufs=4))
-        outp = ctx.enter_context(tc.tile_pool(name="outp", bufs=3))
+        outp = ctx.enter_context(tc.tile_pool(name="outp", bufs=4))
         ps_t = ctx.enter_context(tc.psum_pool(name="ps_t", bufs=4))
         ps_a = ctx.enter_context(tc.psum_pool(name="ps_a", bufs=2))
         ps_q = ctx.enter_context(tc.psum_pool(name="ps_q", bufs=2))
@@ -227,18 +227,19 @@ def tile_extendedanfis_kernel(tc, x, mfs, rules, out):
         r4q = {}
         r4s = {}
 
-        def r4_mm(j, alone=False):
+        def r4_mm(j, u, alone=False):
             if j < NT:
-                if alone or j % 2 == 0:
-                    q = ps_q.tile([P, 1 if alone else 2, R4], F32, tag="q")
-                    r4q[j] = (q, 0)
-                else:
-                    r4q[j] = (r4q[j - 1][0], 1)
+                if u == 0:
+                    if alone or j % 2 == 0:
+                        q = ps_q.tile([P, 1 if alone else 2, 2, R4 // 2], F32, tag="q")
+                        r4q[j] = (q, 0)
+                    else:
+                        r4q[j] = (r4q[j - 1][0], 1)
                 q, k = r4q[j]
                 nc.tensor.matmul(
-                    out=q[:, k, :],
+                    out=q[:, k, u, :],
                     lhsT=feat[:, j // GT, :],
-                    rhs=selr[:, j % GT, :, :].rearrange("p a c -> p (a c)"),
+                    rhs=selr[:, j % GT, 8 * u : 8 * u + 8, :].rearrange("p a c -> p (a c)"),
                     start=True,
                     stop=True,
                 )
@@ -250,7 +251,7 @@ def tile_extendedanfis_kernel(tc, x, mfs, rules, out):
                     r4s[j // 2] = r4
                 nc.scalar.activation(
                     out=r4s[j // 2][:, j % 2 : j % 2 + n, :].rearrange("p j k -> p (j k)"),
-                    in_=r4q[j][0][:].rearrange("p j k -> p (j k)"),
+                    in_=r4q[j][0][:].rearrange("p j u k -> p (j u k)"),
                     func=ACT.Exp,
                     scale=-0.5,
                 )
@@ -367,10 +368,12 @@ def tile_extendedanfis_kernel(tc, x, mfs, rules, out):
         rules_regroup(0, nc.scalar.copy)
         small_mm(0)
         small_exp(0)
-        r4_mm(0, alone=True)
+        for u in range(2):
+            r4_mm(0, u, alone=True)
         r4_exp(0, 1)
         replicate(1, 4)
-        r4_mm(1, alone=True)
+        for u in range(2):
+            r4_mm(1, u, alone=True)
         for op in small_chain(0):
             op()
         for q in range(4):
@@ -378,8 +381,9 @@ def tile_extendedanfis_kernel(tc, x, mfs, rules, out):
         r4_exp(1, 1)
         xq1 = xtrans(1, 4, ps_t, "xt")
         square(1, 4, xq1)
-        r4_mm(2)
-        r4_mm(3)
+        for j in (2, 3):
+            for u in range(2):
+                r4_mm(j, u)
         small_mm(1)
 
         mm_step = {}
@@ -398,6 +402,7 @@ def tile_extendedanfis_kernel(tc, x, mfs, rules, out):
                 fill.extend(small_chain(chain_step[s]))
             evac(s - 2, 1)
             trans(s - 1, 0)
+            r4_mm(s + 4, 0)
             gen_v(s, 0)
             pop(2 if s < 4 else 1)
             gen_s(s + 1, 0)
@@ -422,7 +427,7 @@ def tile_extendedanfis_kernel(tc, x, mfs, rules, out):
             gen_v(s, 2)
             pop(2 if s < 4 else 1)
             gen_s(s + 1, 2)
-            r4_mm(s + 4)
+            r4_mm(s + 4, 1)
 
             evac(s - 1, 0)
             trans(s - 1, 3)

@@ -67,13 +67,9 @@ def tile_extendedanfis_kernel(tc, x, mfs, rules, out):
             in_=mfs.rearrange("i m c -> (i m c)").partition_broadcast(P),
         )
         rraw = const.tile([P, PASSES, 4, O], BF16)
-        rules_v = rules.rearrange("(z a y q w) o -> z y a q (w o)", z=M, y=M, q=8, w=2)
-        for z in range(M):
-            for y in range(M):
-                nc.sync.dma_start(
-                    out=rraw[:, 2 * z + y // 2, 2 * (y % 2) : 2 * (y % 2) + 2, :].rearrange("p w o -> p (w o)"),
-                    in_=rules_v[z, y],
-                )
+        rules_v = rules.rearrange("(g p t) o -> p g t o", p=P, t=4)
+        for k in range(4):
+            nc.sync.dma_start(out=rraw[:, 2 * k : 2 * k + 2, :, :], in_=rules_v[:, 2 * k : 2 * k + 2, :, :])
 
         xrep = const.tile([P, NG, P], BF16, align_bytes=64)
         nc.vector.memset(xrep[:, :, GT * IM :], 0.0)
@@ -85,9 +81,9 @@ def tile_extendedanfis_kernel(tc, x, mfs, rules, out):
         row = ident[:, : GT * IM].rearrange("p (j i m) -> p j i m", j=GT, i=I)
         sq = [P, GT, M, M]
         sels = const.tile([P, GT, SM], F32)
-        a12 = const.tile(sq, F32)
-        a45 = const.tile(sq, F32)
-        selr = const.tile([P, GT, 16, 16], F32)
+        a23 = const.tile(sq, F32)
+        a45 = const.tile([P, GT, 2, M, 2], F32)
+        selr = const.tile([P, GT, 2, 16, 8], F32)
 
         def add(dst, a, b):
             nc.vector.tensor_tensor(out=dst, in0=a, in1=b, op=ALU.add)
@@ -96,18 +92,26 @@ def tile_extendedanfis_kernel(tc, x, mfs, rules, out):
             add(dst, row[:, :, i, :].unsqueeze(3).to_broadcast(sq), row[:, :, k, :].unsqueeze(2).to_broadcast(sq))
 
         def selr_part(j0):
-            shp = [P, 2, 16, 16]
-            add(
-                selr[:, j0 : j0 + 2, :, :],
-                a12[:, j0 : j0 + 2, :, :].rearrange("p j a b -> p j (a b)").unsqueeze(3).to_broadcast(shp),
-                a45[:, j0 : j0 + 2, :, :].rearrange("p j a b -> p j (a b)").unsqueeze(2).to_broadcast(shp),
-            )
+            shp = [P, 2, 16, 8]
+            for u in range(2):
+                add(
+                    selr[:, j0 : j0 + 2, u, :, :],
+                    a23[:, j0 : j0 + 2, :, :].rearrange("p j a b -> p j (a b)").unsqueeze(3).to_broadcast(shp),
+                    a45[:, j0 : j0 + 2, u, :, :].rearrange("p j a b -> p j (a b)").unsqueeze(2).to_broadcast(shp),
+                )
 
-        outer(sels[:, :, :S16].rearrange("p j (a b) -> p j a b", a=M), 0, 3)
+        outer(sels[:, :, :S16].rearrange("p j (a b) -> p j a b", a=M), 0, 1)
         nc.vector.tensor_copy(out=sels[:, :, S16:], in_=ident[:, : GT * IM].rearrange("p (j f) -> p j f", j=GT))
-        outer(a12[:], 1, 2)
-        outer(a45[:], 4, 5)
+        outer(a23[:], 2, 3)
+        for u in range(2):
+            shp = [P, GT, M, 2]
+            add(
+                a45[:, :, u, :, :],
+                row[:, :, 4, :].unsqueeze(3).to_broadcast(shp),
+                row[:, :, 5, 2 * u : 2 * u + 2].unsqueeze(2).to_broadcast(shp),
+            )
         selr_part(0)
+        selr_part(2)
 
         sg = const.tile([P, IM], F32)
         rsb = const.tile([P, 2, IM], F32)
@@ -239,7 +243,7 @@ def tile_extendedanfis_kernel(tc, x, mfs, rules, out):
                 nc.tensor.matmul(
                     out=q[:, k, u, :],
                     lhsT=feat[:, j // GT, :],
-                    rhs=selr[:, j % GT, 8 * u : 8 * u + 8, :].rearrange("p a c -> p (a c)"),
+                    rhs=selr[:, j % GT, u, :, :].rearrange("p a c -> p (a c)"),
                     start=True,
                     stop=True,
                 )
@@ -247,10 +251,10 @@ def tile_extendedanfis_kernel(tc, x, mfs, rules, out):
         def r4_exp(j, n):
             if j < NT:
                 if j % 2 == 0:
-                    r4 = tab.tile([P, 2, R4], F32, tag="r4")
+                    r4 = tab.tile([P, 2, 2, R4 // 2], F32, tag="r4")
                     r4s[j // 2] = r4
                 nc.scalar.activation(
-                    out=r4s[j // 2][:, j % 2 : j % 2 + n, :].rearrange("p j k -> p (j k)"),
+                    out=r4s[j // 2][:, j % 2 : j % 2 + n, :, :].rearrange("p j u k -> p (j u k)"),
                     in_=r4q[j][0][:].rearrange("p j u k -> p (j u k)"),
                     func=ACT.Exp,
                     scale=-0.5,
@@ -267,14 +271,14 @@ def tile_extendedanfis_kernel(tc, x, mfs, rules, out):
 
         def nb_tile(j, q):
             if (j, q) not in nbs:
-                nb = nbp.tile([P, 4, R4], BF16, tag="nb%d" % q)
+                nb = nbp.tile([P, 2, 2, 2, R4 // 2], BF16, tag="nb%d" % q)
                 nbs[(j, q)] = nb
             return nbs[(j, q)]
 
         def gen_one(j, h, on_scalar):
             nb = nb_tile(j, h // 4)
-            dst = nb[:, h % 4, :]
-            src = r4s[j // 2][:, j % 2, :]
+            dst = nb[:, (h // 2) % 2, :, h % 2, :]
+            src = r4s[j // 2][:, j % 2, :, :]
             c = chunk_of[j]
             sc = s16s[c][:, j - starts[c], h : h + 1]
             if on_scalar:
@@ -296,7 +300,7 @@ def tile_extendedanfis_kernel(tc, x, mfs, rules, out):
 
         def trans(j, q):
             if ok(j):
-                nbw = nbs[(j, q)][:].rearrange("p h c -> p (h c)").bitcast(F32)
+                nbw = nbs[(j, q)][:].rearrange("p g u s c -> p (g u s c)").bitcast(F32)
                 xt = ps_t.tile([P, 4, P], F32, tag="xt")
                 for r in range(4):
                     nc.tensor.transpose(xt[:, r, :], nbw[:, r * P : (r + 1) * P], ident[:])
@@ -362,7 +366,6 @@ def tile_extendedanfis_kernel(tc, x, mfs, rules, out):
         replicate(0, 1)
         row_constants()
         row_select()
-        selr_part(2)
         xq0 = xtrans(0, 1, ps_q, "q")
         square(0, 1, xq0)
         rules_regroup(0, nc.scalar.copy)
@@ -371,7 +374,7 @@ def tile_extendedanfis_kernel(tc, x, mfs, rules, out):
         for u in range(2):
             r4_mm(0, u, alone=True)
         r4_exp(0, 1)
-        replicate(1, 4)
+        replicate(1, NG)
         for u in range(2):
             r4_mm(1, u, alone=True)
         for op in small_chain(0):
@@ -441,5 +444,4 @@ def tile_extendedanfis_kernel(tc, x, mfs, rules, out):
                 rules_regroup(s, nc.vector.tensor_copy)
             if s in late:
                 g0, g1 = late[s]
-                replicate(g0, g1)
                 square(g0, g1, xtrans(g0, g1, ps_t, "xt"))

@@ -34,7 +34,7 @@ def scalar_share(j):
         return ((7, 15), (7,), ())[j - NT + 3]
     if j == 0:
         return (3, 7, 11, 15)
-    return (7, 15) if j % 2 else (3, 7, 15)
+    return (3, 7, 15) if j % 5 % 2 == 0 else (7, 15)
 
 
 def tile_extendedanfis_kernel(tc, x, mfs, rules, out):

from contextlib import ExitStack

import concourse.mybir as mybir
from concourse.masks import make_identity

F32 = mybir.dt.float32
BF16 = mybir.dt.bfloat16
U32 = mybir.dt.uint32
U8 = mybir.dt.uint8
FP8X4 = mybir.dt.float8_e4m3fn_x4
ALU = mybir.AluOpType
ACT = mybir.ActivationFunctionType
AX = mybir.AxisListType

P = 128
B, I, M, O = 8192, 6, 4, 128
R = M ** I
NT = B // P
IM = I * M
GT = 4
NG = NT // GT
S16 = M * M
SM = S16 + IM
R4 = M ** 4
CHUNKS = (4, 12, 12, 12, 12, 12)
ACCS = (4,) * 15 + (2, 1, 1)
PASSES = R // 512
EPS = 1e-6
FLOPS = 2 * B * R * O


def scalar_share(j):
    if j >= NT - 3:
        return ((7, 15), (7,), ())[j - NT + 3]
    if j == 0:
        return (3, 7, 11, 15)
    return (3, 7, 15) if j % 5 % 2 == 0 else (7, 15)


def tile_extendedanfis_kernel(tc, x, mfs, rules, out):
    nc = tc.nc
    starts = [sum(CHUNKS[:c]) for c in range(len(CHUNKS))]
    chunk_of = []
    for c in range(len(CHUNKS)):
        chunk_of.extend([c] * CHUNKS[c])
    acc_starts = [sum(ACCS[:c]) for c in range(len(ACCS))]
    acc_of = []
    for c in range(len(ACCS)):
        acc_of.extend([c] * ACCS[c])
    with ExitStack() as ctx:
        ctx.enter_context(tc.manual_schedule())
        const = ctx.enter_context(tc.tile_pool(name="const", bufs=1))
        tab = ctx.enter_context(tc.tile_pool(name="tab", bufs=3))
        nbp = ctx.enter_context(tc.tile_pool(name="nbp", bufs=4))
        grpp = ctx.enter_context(tc.tile_pool(name="grpp", bufs=4))
        qp = ctx.enter_context(tc.tile_pool(name="qp", bufs=4))
        outp = ctx.enter_context(tc.tile_pool(name="outp", bufs=4))
        ps_t = ctx.enter_context(tc.psum_pool(name="ps_t", bufs=4))
        ps_a = ctx.enter_context(tc.psum_pool(name="ps_a", bufs=2))
        ps_q = ctx.enter_context(tc.psum_pool(name="ps_q", bufs=2))

        x_sb = const.tile([P, NT, I], BF16)
        nc.sync.dma_start(out=x_sb[:], in_=x.rearrange("(p j) i -> p j i", j=NT))
        mfb = const.tile([P, IM, 2], BF16)
        nc.scalar.dma_start(
            out=mfb[:].rearrange("p f c -> p (f c)"),
            in_=mfs.rearrange("i m c -> (i m c)").partition_broadcast(P),
        )
        rraw = const.tile([P, PASSES, 4, O], BF16)
        rules_v = rules.rearrange("(g p t) o -> p g t o", p=P, t=4)
        for k in range(4):
            nc.sync.dma_start(out=rraw[:, 2 * k : 2 * k + 2, :, :], in_=rules_v[:, 2 * k : 2 * k + 2, :, :])

        xrep = const.tile([P, NG, P], BF16, align_bytes=64)
        nc.vector.memset(xrep[:, :, GT * IM :], 0.0)
        ident = const.tile([P, P], F32)
        make_identity(nc, ident[:])
        identb = const.tile([P, P], BF16, align_bytes=64)
        nc.vector.tensor_copy(out=identb[:], in_=ident[:])

        row = ident[:, : GT * IM].rearrange("p (j i m) -> p j i m", j=GT, i=I)
        sq = [P, GT, M, M]
        sels = const.tile([P, GT, SM], F32)
        a23 = const.tile(sq, F32)
        a45 = const.tile([P, GT, 2, M, 2], F32)
        selr = const.tile([P, GT, 2, 16, 8], F32)

        def add(dst, a, b):
            nc.vector.tensor_tensor(out=dst, in0=a, in1=b, op=ALU.add)

        def outer(dst, i, k):
            add(dst, row[:, :, i, :].unsqueeze(3).to_broadcast(sq), row[:, :, k, :].unsqueeze(2).to_broadcast(sq))

        def selr_part(j0):
            shp = [P, 2, 16, 8]
            for u in range(2):
                add(
                    selr[:, j0 : j0 + 2, u, :, :],
                    a23[:, j0 : j0 + 2, :, :].rearrange("p j a b -> p j (a b)").unsqueeze(3).to_broadcast(shp),
                    a45[:, j0 : j0 + 2, u, :, :].rearrange("p j a b -> p j (a b)").unsqueeze(2).to_broadcast(shp),
                )

        outer(sels[:, :, :S16].rearrange("p j (a b) -> p j a b", a=M), 0, 1)
        nc.vector.tensor_copy(out=sels[:, :, S16:], in_=ident[:, : GT * IM].rearrange("p (j f) -> p j f", j=GT))
        outer(a23[:], 2, 3)
        for u in range(2):
            shp = [P, GT, M, 2]
            add(
                a45[:, :, u, :, :],
                row[:, :, 4, :].unsqueeze(3).to_broadcast(shp),
                row[:, :, 5, 2 * u : 2 * u + 2].unsqueeze(2).to_broadcast(shp),
            )
        selr_part(0)
        selr_part(2)

        sg = const.tile([P, IM], F32)
        rsb = const.tile([P, 2, IM], F32)
        rsel = const.tile([P, 2, GT, IM], F32)
        rows = const.tile([P, 2, 1], F32)

        def row_constants():
            nc.vector.scalar_tensor_tensor(
                out=sg[:], in0=mfb[:, :, 1], scalar=-1.0, in1=mfb[:, :, 1], op0=ALU.mult, op1=ALU.max
            )
            nc.vector.tensor_scalar_add(out=sg[:], in0=sg[:], scalar1=EPS)
            nc.vector.reciprocal(out=rsb[:, 0, :], in_=sg[:])
            nc.vector.scalar_tensor_tensor(
                out=rsb[:, 1, :], in0=mfb[:, :, 0], scalar=-1.0, in1=rsb[:, 0, :], op0=ALU.mult, op1=ALU.mult
            )

        def row_select():
            shp = [P, 2, GT, IM]
            nc.vector.tensor_tensor(
                out=rsel[:],
                in0=ident[:, : GT * IM].rearrange("p (j f) -> p j f", j=GT).unsqueeze(1).to_broadcast(shp),
                in1=rsb[:].unsqueeze(2).to_broadcast(shp),
                op=ALU.mult,
            )
            nc.vector.tensor_reduce(
                out=rows[:, :, 0], in_=rsel[:].rearrange("p c j f -> p c (j f)"), axis=AX.X, op=ALU.add
            )

        out_v = out.rearrange("(p j) o -> p j o", j=NT)

        rgrp = const.tile([P, PASSES, O, 4], BF16, align_bytes=64)
        rcodes = const.tile([P, PASSES * O], U32, align_bytes=64)
        rscl = const.tile([P, PASSES * O], U8, align_bytes=64)

        def rules_regroup(k, copy):
            g = 2 * k
            copy(
                out=rgrp[:, g : g + 2, :, :], in_=rraw[:, g : g + 2, :, :].rearrange("p g t o -> p g o t")
            )

        def rules_quant():
            nc.vector.quantize_mx(
                out=rcodes[:].bitcast(FP8X4), scales=rscl[:], in_=rgrp[:].rearrange("p g o t -> p (g o t)")
            )

        feat = const.tile([P, NG, P], F32)

        def replicate(g0, g1):
            n = g1 - g0
            nc.vector.tensor_copy(
                out=xrep[:, g0:g1, : GT * IM].rearrange("p g (f m) -> p g f m", m=M),
                in_=x_sb[:, GT * g0 : GT * g1, :]
                .rearrange("p (g j) i -> p g (j i)", j=GT)
                .unsqueeze(3)
                .to_broadcast([P, n, GT * I, M]),
            )

        def xtrans(g0, g1, pool, tag):
            n = g1 - g0
            xq = pool.tile([P, n, P], BF16, tag=tag)
            for g in range(g0, g1):
                nc.tensor.transpose(xq[:, g - g0, :], xrep[:, g, :], identb[:])
            return xq

        def square(g0, g1, xq):
            nc.scalar.activation(
                out=feat[:, g0:g1, :], in_=xq[:], func=ACT.Square, scale=rows[:, 0, :], bias=rows[:, 1, :]
            )

        smq = {}
        sms = {}
        s16s = {}

        def small_mm(c):
            ng = CHUNKS[c] // GT
            q = ps_q.tile([P, ng, GT * SM], F32, tag="q")
            for k in range(ng):
                nc.tensor.matmul(
                    out=q[:, k, :],
                    lhsT=feat[:, starts[c] // GT + k, :],
                    rhs=sels[:].rearrange("p j k -> p (j k)"),
                    start=True,
                    stop=True,
                )
            smq[c] = q

        def small_exp(c):
            sm = tab.tile([P, CHUNKS[c], SM], F32, tag="sm")
            nc.scalar.activation(
                out=sm[:].rearrange("p j k -> p (j k)"),
                in_=smq[c][:].rearrange("p g k -> p (g k)"),
                func=ACT.Exp,
                scale=-0.5,
            )
            sms[c] = sm

        def small_chain(c):
            nj = CHUNKS[c]
            sm = sms[c]
            ssum = tab.tile([P, nj, I], F32, tag="ssum")
            den = tab.tile([P, nj, 1], F32, tag="den")
            rn = tab.tile([P, nj, 1], F32, tag="rn")
            s16 = tab.tile([P, nj, S16], F32, tag="s16")
            s16s[c] = s16
            return [
                lambda: nc.vector.tensor_reduce(
                    out=ssum[:], in_=sm[:, :, S16:].rearrange("p j (i m) -> p j i m", m=M), axis=AX.X, op=ALU.add
                ),
                lambda: nc.vector.tensor_reduce(out=den[:], in_=ssum[:], axis=AX.X, op=ALU.mult),
                lambda: nc.vector.tensor_scalar_add(out=den[:], in0=den[:], scalar1=EPS),
                lambda: nc.vector.reciprocal(out=rn[:], in_=den[:]),
                lambda: nc.vector.tensor_tensor(
                    out=s16[:], in0=sm[:, :, :S16], in1=rn[:].to_broadcast([P, nj, S16]), op=ALU.mult
                ),
            ]

        r4q = {}
        r4s = {}

        def r4_mm(j, u, alone=False):
            if j < NT:
                if u == 0:
                    if alone or j % 2 == 0:
                        q = ps_q.tile([P, 1 if alone else 2, 2, R4 // 2], F32, tag="q")
                        r4q[j] = (q, 0)
                    else:
                        r4q[j] = (r4q[j - 1][0], 1)
                q, k = r4q[j]
                nc.tensor.matmul(
                    out=q[:, k, u, :],
                    lhsT=feat[:, j // GT, :],
                    rhs=selr[:, j % GT, u, :, :].rearrange("p a c -> p (a c)"),
                    start=True,
                    stop=True,
                )

        def r4_exp(j, n):
            if j < NT:
                if j % 2 == 0:
                    r4 = tab.tile([P, 2, 2, R4 // 2], F32, tag="r4")
                    r4s[j // 2] = r4
                nc.scalar.activation(
                    out=r4s[j // 2][:, j % 2 : j % 2 + n, :, :].rearrange("p j u k -> p (j u k)"),
                    in_=r4q[j][0][:].rearrange("p j u k -> p (j u k)"),
                    func=ACT.Exp,
                    scale=-0.5,
                )

        nbs = {}
        xts = {}
        grps = {}
        qs = {}
        accs = {}

        def ok(j):
            return 0 <= j < NT

        def nb_tile(j, q):
            if (j, q) not in nbs:
                nb = nbp.tile([P, 2, 2, 2, R4 // 2], BF16, tag="nb%d" % q)
                nbs[(j, q)] = nb
            return nbs[(j, q)]

        def gen_one(j, h, on_scalar):
            nb = nb_tile(j, h // 4)
            dst = nb[:, (h // 2) % 2, :, h % 2, :]
            src = r4s[j // 2][:, j % 2, :, :]
            c = chunk_of[j]
            sc = s16s[c][:, j - starts[c], h : h + 1]
            if on_scalar:
                nc.scalar.activation(out=dst, in_=src, func=ACT.Copy, scale=sc)
            else:
                nc.vector.tensor_scalar_mul(out=dst, in0=src, scalar1=sc)

        def gen_v(j, q):
            if ok(j):
                for h in range(4 * q, 4 * q + 4):
                    if h not in scalar_share(j):
                        gen_one(j, h, False)

        def gen_s(j, q):
            if ok(j):
                for h in range(4 * q, 4 * q + 4):
                    if h in scalar_share(j):
                        gen_one(j, h, True)

        def trans(j, q):
            if ok(j):
                nbw = nbs[(j, q)][:].rearrange("p g u s c -> p (g u s c)").bitcast(F32)
                xt = ps_t.tile([P, 4, P], F32, tag="xt")
                for r in range(4):
                    nc.tensor.transpose(xt[:, r, :], nbw[:, r * P : (r + 1) * P], ident[:])
                xts[(j, q)] = xt

        def evac(j, q):
            if ok(j):
                if q == 0:
                    grp = grpp.tile([P, PASSES * P * 4], BF16, tag="grp", align_bytes=64)
                    grps[j] = grp
                gw = grps[j][:].bitcast(F32).rearrange("p (g b u) -> p g b u", g=PASSES, u=2)
                nc.scalar.copy(
                    out=gw[:, 2 * q : 2 * q + 2, :, :], in_=xts[(j, q)][:].rearrange("p (g u) b -> p g b u", u=2)
                )

        def quant(j):
            if ok(j):
                codes = qp.tile([P, PASSES * P], U32, tag="codes", align_bytes=64)
                scl = qp.tile([P, PASSES * P], U8, tag="scl", align_bytes=64)
                pieces = 2 if j == NT - 1 else 1
                wid = PASSES * P // pieces
                for k in range(pieces):
                    nc.vector.quantize_mx(
                        out=codes[:, k * wid : (k + 1) * wid].bitcast(FP8X4),
                        scales=scl[:, k * wid : (k + 1) * wid],
                        in_=grps[j][:, 4 * k * wid : 4 * (k + 1) * wid],
                    )
                qs[j] = (codes, scl)

        def mx(j, part):
            if ok(j):
                codes, scl = qs[j]
                c = acc_of[j]
                if j == acc_starts[c] and part == 0:
                    acc = ps_a.tile([P, ACCS[c], O], F32, tag="acc")
                    accs[c] = acc
                for g in range(part * PASSES // 2, (part + 1) * PASSES // 2):
                    nc.tensor.matmul_mx(
                        out=accs[c][:, j - acc_starts[c], :],
                        lhsT=codes[:, g * P : (g + 1) * P].bitcast(FP8X4),
                        lhsT_scale=scl[:, g * P : (g + 1) * P],
                        rhs=rcodes[:, g * O : (g + 1) * O].bitcast(FP8X4),
                        rhs_scale=rscl[:, g * O : (g + 1) * O],
                        start=(g == 0),
                        stop=(g == PASSES - 1),
                    )

        def outcopy(j):
            if ok(j):
                c = acc_of[j]
                if j == acc_starts[c] + ACCS[c] - 1:
                    osb = outp.tile([P, ACCS[c], O], F32, tag="osb")
                    nc.scalar.copy(out=osb[:], in_=accs[c][:])
                    nc.sync.dma_start(out=out_v[:, acc_starts[c] : acc_starts[c] + ACCS[c], :], in_=osb[:])

        fill = []

        def pop(n):
            for op in fill[:n]:
                op()
            fill[:n] = []

        replicate(0, 1)
        row_constants()
        row_select()
        xq0 = xtrans(0, 1, ps_q, "q")
        square(0, 1, xq0)
        rules_regroup(0, nc.scalar.copy)
        small_mm(0)
        small_exp(0)
        for u in range(2):
            r4_mm(0, u, alone=True)
        r4_exp(0, 1)
        replicate(1, NG)
        for u in range(2):
            r4_mm(1, u, alone=True)
        for op in small_chain(0):
            op()
        for q in range(4):
            gen_s(0, q)
        r4_exp(1, 1)
        xq1 = xtrans(1, 4, ps_t, "xt")
        square(1, 4, xq1)
        for j in (2, 3):
            for u in range(2):
                r4_mm(j, u)
        small_mm(1)

        mm_step = {}
        exp_step = {}
        chain_step = {2: 1}
        exp_step[0] = 1
        late = {0: (4, 10), 1: (10, NG)}
        for c in range(2, len(CHUNKS)):
            mm_step[starts[c] - 7] = c
            exp_step[starts[c] - 5] = c
            chain_step[starts[c] - 4] = c

        for s in range(NT + 7):
            if s in chain_step:
                assert len(fill) == 0
                fill.extend(small_chain(chain_step[s]))
            evac(s - 2, 1)
            trans(s - 1, 0)
            r4_mm(s + 4, 0)
            gen_v(s, 0)
            pop(2 if s < 4 else 1)
            gen_s(s + 1, 0)
            if s % 2 == 0:
                r4_exp(s + 2, 2)
            outcopy(s - 6)

            evac(s - 2, 2)
            trans(s - 1, 1)
            mx(s - 5, 0)
            gen_v(s, 1)
            pop(2 if s < 4 else 1)
            gen_s(s + 1, 1)
            if s in exp_step:
                small_exp(exp_step[s])
            if s == 4:
                rules_quant()
            quant(s - 3)

            evac(s - 2, 3)
            trans(s - 1, 2)
            gen_v(s, 2)
            pop(2 if s < 4 else 1)
            gen_s(s + 1, 2)
            r4_mm(s + 4, 1)

            evac(s - 1, 0)
            trans(s - 1, 3)
            mx(s - 5, 1)
            gen_v(s, 3)
            pop(2 if s < 4 else 1)
            gen_s(s + 1, 3)
            if s in mm_step:
                small_mm(mm_step[s])
            if s in (1, 2, 3):
                rules_regroup(s, nc.vector.tensor_copy)
            if s in late:
                g0, g1 = late[s]
                square(g0, g1, xtrans(g0, g1, ps_t, "xt"))
